import numpy as np
import ml_dtypes

BF16 = ml_dtypes.bfloat16


def bf(x):
    return np.asarray(x, np.float32).astype(BF16)


def f32(x):
    return np.asarray(x, np.float32)


def f64(x):
    return np.asarray(x).astype(np.float64)


def striped(idx):
    return np.tile(idx.reshape(-1, 16).T, (8, 1))


D, K, N = 128, 256, 1024
LAMBDA_ENERGY = 0.1


def sigmoid(v):
    return 1.0 / (1.0 + np.exp(-v))


def setup_inputs():
    return {"z_real": bf(3.0 * np.random.standard_normal((D, N))), "z_imag": bf(3.0 * np.random.standard_normal((D, N))), "codebook": bf(3.0 * np.random.standard_normal((K, 2 * D))), "adj_t": f32(2.0 * np.random.standard_normal((K, K))), "offs": striped(np.concatenate([np.random.permutation(K) for _ in range(-(-(N) // K))])[:N])}


def reference(z_real, z_imag, codebook, adj_t, offs):
    idx = offs[:16].T.reshape(-1)
    zr, zi, cb = f64(z_real), f64(z_imag), f64(codebook)
    mag = np.sqrt(zr * zr + zi * zi)
    var = np.sum((mag - np.mean(mag)) ** 2) / (mag.size - 1)
    g = LAMBDA_ENERGY * np.log(1.0 + np.exp(var))
    z = np.concatenate([zr, zi], axis=0)
    dist = (np.sum(cb * cb, axis=1, keepdims=True) - 2.0 * (cb @ z)) / (2 * D)
    logits = g * sigmoid(f64(adj_t))[:, idx] - dist
    e = np.exp(logits - logits.max(axis=0, keepdims=True))
    probs = e / e.sum(axis=0, keepdims=True)
    return cb[:, :D].T @ probs

@@ -1,0 +1,166 @@
+import concourse.mybir as mybir
+from concourse.masks import make_identity
+
+F32 = mybir.dt.float32
+BF16 = mybir.dt.bfloat16
+U16 = mybir.dt.uint16
+ALU = mybir.AluOpType
+ACT = mybir.ActivationFunctionType
+AX = mybir.AxisListType
+
+P = 128
+D, K, N = 128, 256, 1024
+KB = K // P
+PIECE = 256
+SUBS = PIECE // P
+BANK = 512
+HALF = N // 2
+COUNT = D * N
+EULER = 2.718281828459045
+
+FLOPS = 2 * K * 2 * D * N + 2 * K * D * N
+
+
+def tile_mirrorsystem_kernel(tc, z_real, z_imag, codebook, adj_t, offs, out):
+    nc = tc.nc
+    with (
+        tc.tile_pool(name="held", bufs=1) as held,
+        tc.tile_pool(name="work", bufs=2) as work,
+        tc.tile_pool(name="small", bufs=2) as small,
+    ):
+        offsets = held.tile([P, N // 16], U16, name="offsets")
+        nc.sync.dma_start(offsets[:], offs)
+        adj = held.tile([P, KB, K], F32, name="adj")
+        nc.scalar.dma_start(adj[:], adj_t.rearrange("(b p) n -> p b n", p=P))
+        zr = held.tile([P, N], BF16, name="zr")
+        nc.sync.dma_start(zr[:], z_real)
+        zi = held.tile([P, N], BF16, name="zi")
+        nc.sync.dma_start(zi[:], z_imag)
+        codes = held.tile([P, KB, 2 * D], BF16, name="codes")
+        nc.scalar.dma_start(codes[:], codebook.rearrange("(b p) e -> p b e", p=P))
+
+        ident_f = held.tile([P, P], F32, name="ident_f")
+        make_identity(nc, ident_f[:])
+        ident_b = held.tile([P, P], BF16, name="ident_b")
+        make_identity(nc, ident_b[:])
+        averager = held.tile([P, P], F32, name="averager")
+        nc.vector.memset(averager[:], 1.0 / COUNT)
+        euler = held.tile([P, 1], F32, name="euler")
+        nc.vector.memset(euler[:], EULER)
+
+        sig = held.tile([P, KB, K], F32, name="sig")
+        nc.scalar.activation(sig[:], adj[:], ACT.Sigmoid)
+
+        neg_dist = [held.tile([P, N], F32, name=f"neg_dist{kb}") for kb in range(KB)]
+        mean_mag = held.tile([P, 1], F32, name="mean_mag")
+        mean_sq = held.tile([P, 1], F32, name="mean_sq")
+        with tc.psum_pool(name="psum_pre", bufs=1) as psum_pre:
+            codes_t_ps = psum_pre.tile([P, 2, K], BF16, name="codes_t_ps")
+            for kb in range(KB):
+                for half in range(2):
+                    nc.tensor.transpose(
+                        codes_t_ps[:, half, kb * P : (kb + 1) * P], codes[:, kb, half * D : (half + 1) * D], ident_b[:]
+                    )
+            codes_t = held.tile([P, 2, K], BF16, name="codes_t")
+            nc.scalar.copy(codes_t[:], codes_t_ps[:])
+            code_sq = held.tile([P, KB, 2 * D], F32, name="code_sq")
+            norm = held.tile([P, KB], F32, name="norm")
+            for kb in range(KB):
+                nc.scalar.activation(
+                    code_sq[:, kb, :], codes[:, kb, :], ACT.Square, scale=1.0 / 16.0, accum_out=norm[:, kb : kb + 1]
+                )
+
+            sq_r = held.tile([P, N], F32, name="sq_r")
+            sq_i = held.tile([P, N], F32, name="sq_i")
+            mag_sq = held.tile([P, N], F32, name="mag_sq")
+            mag = held.tile([P, N], F32, name="mag")
+            sum_sq = held.tile([P, 2], F32, name="sum_sq")
+            sum_mag = held.tile([P, 2], F32, name="sum_mag")
+            for h in range(2):
+                cols = slice(h * HALF, (h + 1) * HALF)
+                nc.gpsimd.tensor_tensor(sq_r[:, cols], zr[:, cols], zr[:, cols], ALU.mult)
+                nc.vector.tensor_tensor(sq_i[:, cols], zi[:, cols], zi[:, cols], ALU.mult)
+                nc.vector.scalar_tensor_tensor(
+                    mag_sq[:, cols], sq_r[:, cols], 1.0, sq_i[:, cols], ALU.mult, ALU.add, accum_out=sum_sq[:, h : h + 1]
+                )
+                nc.scalar.activation(mag[:, cols], mag_sq[:, cols], ACT.Sqrt, accum_out=sum_mag[:, h : h + 1])
+
+            for c in range(N // BANK):
+                cols = slice(c * BANK, (c + 1) * BANK)
+                for kb in range(KB):
+                    score = psum_pre.tile([P, BANK], F32, name="score", bufs=4)
+                    nc.tensor.matmul(score[:], codes_t[:, 0, kb * P : (kb + 1) * P], zr[:, cols], start=True, stop=False)
+                    nc.tensor.matmul(score[:], codes_t[:, 1, kb * P : (kb + 1) * P], zi[:, cols], start=False, stop=True)
+                    nc.vector.tensor_scalar(
+                        neg_dist[kb][:, cols], score[:], 1.0 / 128.0, norm[:, kb : kb + 1], ALU.mult, ALU.subtract
+                    )
+
+            mean_sq_ps = psum_pre.tile([P, 1], F32, name="mean_sq_ps")
+            mean_mag_ps = psum_pre.tile([P, 1], F32, name="mean_mag_ps")
+            for h in range(2):
+                nc.tensor.matmul(mean_sq_ps[:], averager[:], sum_sq[:, h : h + 1], start=(h == 0), stop=(h == 1))
+            nc.vector.tensor_copy(mean_sq[:], mean_sq_ps[:])
+            for h in range(2):
+                nc.tensor.matmul(mean_mag_ps[:], averager[:], sum_mag[:, h : h + 1], start=(h == 0), stop=(h == 1))
+            nc.vector.tensor_copy(mean_mag[:], mean_mag_ps[:])
+
+        neg_var = held.tile([P, 1], F32, name="neg_var")
+        nc.vector.tensor_scalar(neg_var[:], mean_mag[:], mean_mag[:, 0:1], mean_sq[:, 0:1], ALU.mult, ALU.subtract)
+        nc.vector.tensor_scalar_mul(neg_var[:], neg_var[:], COUNT / (COUNT - 1.0))
+        exp_neg = held.tile([P, 1], F32, name="exp_neg")
+        nc.gpsimd.tensor_tensor(exp_neg[:], euler[:], neg_var[:], ALU.pow)
+        log_term = held.tile([P, 1], F32, name="log_term")
+        nc.scalar.activation(log_term[:], exp_neg[:], ACT.Ln, bias=1.0)
+        gam = held.tile([P, 1], F32, name="gam")
+        nc.vector.tensor_scalar(gam[:], log_term[:], neg_var[:, 0:1], 0.1, ALU.subtract, ALU.mult)
+
+        gate = [held.tile([P, K], F32, name=f"gate{kb}") for kb in range(KB)]
+        for kb in range(KB):
+            nc.vector.tensor_scalar_mul(gate[kb][:], sig[:, kb, :], gam[:, 0:1])
+
+        with (
+            tc.psum_pool(name="psum_t", bufs=2) as psum_t,
+            tc.psum_pool(name="psum_b", bufs=2) as psum_b,
+            tc.psum_pool(name="psum_o", bufs=2) as psum_o,
+        ):
+            for c in range(N // PIECE):
+                cols = slice(c * PIECE, (c + 1) * PIECE)
+                piece_offsets = offsets[:, c * (PIECE // 16) : (c + 1) * (PIECE // 16)]
+                logits = [work.tile([P, PIECE], F32, name=f"logits{kb}") for kb in range(KB)]
+                for kb in range(KB):
+                    nc.vector.tensor_tensor(
+                        logits[kb][:], gate[kb][:].indirect(piece_offsets), neg_dist[kb][:, cols], ALU.add
+                    )
+                logits_t = psum_t.tile([P, SUBS, K], F32, name="logits_t")
+                for s in range(SUBS):
+                    for kb in range(KB):
+                        nc.tensor.transpose(
+                            logits_t[:, s, kb * P : (kb + 1) * P], logits[kb][:, s * P : (s + 1) * P], ident_f[:]
+                        )
+                neg_max = small.tile([P, SUBS], F32, name="neg_max")
+                nc.vector.tensor_reduce(neg_max[:], logits_t[:], AX.X, ALU.max, negate=True)
+                expo = work.tile([P, SUBS, K], F32, name="expo")
+                denom = small.tile([P, SUBS], F32, name="denom")
+                for s in range(SUBS):
+                    nc.scalar.activation(
+                        expo[:, s, :], logits_t[:, s, :], ACT.Exp, bias=neg_max[:, s : s + 1], accum_out=denom[:, s : s + 1]
+                    )
+                recip = small.tile([P, SUBS], F32, name="recip")
+                nc.vector.reciprocal(recip[:], denom[:])
+                probs_t = work.tile([P, SUBS, K], BF16, name="probs_t")
+                for s in range(SUBS):
+                    nc.vector.tensor_scalar_mul(probs_t[:, s, :], expo[:, s, :], recip[:, s : s + 1])
+                probs_ps = psum_b.tile([P, KB, PIECE], BF16, name="probs_ps")
+                for kb in range(KB):
+                    for s in range(SUBS):
+                        nc.tensor.transpose(
+                            probs_ps[:, kb, s * P : (s + 1) * P], probs_t[:, s, kb * P : (kb + 1) * P], ident_b[:]
+                        )
+                probs = work.tile([P, KB, PIECE], BF16, name="probs")
+                nc.scalar.copy(probs[:], probs_ps[:])
+                quant_ps = psum_o.tile([P, PIECE], F32, name="quant_ps")
+                for kb in range(KB):
+                    nc.tensor.matmul(quant_ps[:], codes[:, kb, 0:D], probs[:, kb, :], start=(kb == 0), stop=(kb == KB - 1))
+                quant = work.tile([P, PIECE], F32, name="quant")
+                nc.scalar.copy(quant[:], quant_ps[:])
+                nc.sync.dma_start(out[:, cols], quant[:])

@@ -16,6 +16,7 @@ SUBS = PIECE // P
 BANK = 512
 HALF = N // 2
 COUNT = D * N
+UNBIAS = COUNT / (COUNT - 1.0)
 EULER = 2.718281828459045
 
 FLOPS = 2 * K * 2 * D * N + 2 * K * D * N
@@ -25,75 +26,99 @@ def tile_mirrorsystem_kernel(tc, z_real, z_imag, codebook, adj_t, offs, out):
     nc = tc.nc
     with (
         tc.tile_pool(name="held", bufs=1) as held,
-        tc.tile_pool(name="work", bufs=2) as work,
-        tc.tile_pool(name="small", bufs=2) as small,
+        tc.tile_pool(name="work", bufs=3) as work,
+        tc.tile_pool(name="small", bufs=4) as small,
     ):
-        offsets = held.tile([P, N // 16], U16, name="offsets")
-        nc.sync.dma_start(offsets[:], offs)
         adj = held.tile([P, KB, K], F32, name="adj")
-        nc.scalar.dma_start(adj[:], adj_t.rearrange("(b p) n -> p b n", p=P))
+        nc.sync.dma_start(adj[:], adj_t.rearrange("(b p) n -> p b n", p=P))
         zr = held.tile([P, N], BF16, name="zr")
-        nc.sync.dma_start(zr[:], z_real)
+        nc.scalar.dma_start(zr[:], z_real)
         zi = held.tile([P, N], BF16, name="zi")
         nc.sync.dma_start(zi[:], z_imag)
         codes = held.tile([P, KB, 2 * D], BF16, name="codes")
         nc.scalar.dma_start(codes[:], codebook.rearrange("(b p) e -> p b e", p=P))
+        offsets = held.tile([P, N // 16], U16, name="offsets")
+        nc.sync.dma_start(offsets[:], offs)
 
-        ident_f = held.tile([P, P], F32, name="ident_f")
-        make_identity(nc, ident_f[:])
         ident_b = held.tile([P, P], BF16, name="ident_b")
         make_identity(nc, ident_b[:])
+        ident_f = held.tile([P, P], F32, name="ident_f")
+        make_identity(nc, ident_f[:])
         averager = held.tile([P, P], F32, name="averager")
         nc.vector.memset(averager[:], 1.0 / COUNT)
         euler = held.tile([P, 1], F32, name="euler")
-        nc.vector.memset(euler[:], EULER)
+        nc.vector.memset(euler[:], EULER**UNBIAS)
 
         sig = held.tile([P, KB, K], F32, name="sig")
-        nc.scalar.activation(sig[:], adj[:], ACT.Sigmoid)
-
-        neg_dist = [held.tile([P, N], F32, name=f"neg_dist{kb}") for kb in range(KB)]
-        mean_mag = held.tile([P, 1], F32, name="mean_mag")
+        codes_t = held.tile([P, 2, K], BF16, name="codes_t")
+        sq_r = held.tile([P, N], F32, name="sq_r")
+        sq_i = held.tile([P, N], F32, name="sq_i")
+        mag_sq = held.tile([P, N], F32, name="mag_sq")
+        mag = held.tile([P, N], F32, name="mag")
+        sum_sq = held.tile([P, 2], F32, name="sum_sq")
+        sum_mag = held.tile([P, 2], F32, name="sum_mag")
+        code_sq = held.tile([P, KB, 2 * D], F32, name="code_sq")
+        neg_norm = held.tile([P, KB], F32, name="neg_norm")
         mean_sq = held.tile([P, 1], F32, name="mean_sq")
+        neg_var = held.tile([P, 1], F32, name="neg_var")
+        tenth_var = held.tile([P, 1], F32, name="tenth_var")
+        exp_neg = held.tile([P, 1], F32, name="exp_neg")
+        log_term = held.tile([P, 1], F32, name="log_term")
+        gam = [held.tile([P, 1], F32, name=f"gam{kb}") for kb in range(KB)]
+        neg_dist = [held.tile([P, N], F32, name=f"neg_dist{kb}") for kb in range(KB)]
+        gate = [held.tile([P, K], F32, name=f"gate{kb}") for kb in range(KB)]
+
+        def squares(h):
+            cols = slice(h * HALF, (h + 1) * HALF)
+            nc.gpsimd.tensor_tensor(sq_r[:, cols], zr[:, cols], zr[:, cols], ALU.mult)
+            nc.vector.tensor_tensor(sq_i[:, cols], zi[:, cols], zi[:, cols], ALU.mult)
+
+        def magnitudes(h):
+            cols = slice(h * HALF, (h + 1) * HALF)
+            nc.vector.scalar_tensor_tensor(
+                mag_sq[:, cols], sq_r[:, cols], 1.0, sq_i[:, cols], ALU.mult, ALU.add, accum_out=sum_sq[:, h : h + 1]
+            )
+            nc.scalar.activation(mag[:, cols], mag_sq[:, cols], ACT.Sqrt, accum_out=sum_mag[:, h : h + 1])
+
+        def code_norm(kb):
+            nc.vector.scalar_tensor_tensor(
+                code_sq[:, kb, :], codes[:, kb, :], -1.0 / 256.0, codes[:, kb, :], ALU.mult, ALU.mult,
+                accum_out=neg_norm[:, kb : kb + 1],
+            )
+
         with tc.psum_pool(name="psum_pre", bufs=1) as psum_pre:
+
+            def scores(c, kb):
+                cols = slice(c * BANK, (c + 1) * BANK)
+                score = psum_pre.tile([P, BANK], F32, name="score", bufs=4)
+                nc.tensor.matmul(score[:], codes_t[:, 0, kb * P : (kb + 1) * P], zr[:, cols], start=True, stop=False)
+                nc.tensor.matmul(score[:], codes_t[:, 1, kb * P : (kb + 1) * P], zi[:, cols], start=False, stop=True)
+                return score
+
+            def negate_on_vector(c, kb, score):
+                nc.vector.tensor_scalar(
+                    neg_dist[kb][:, c * BANK : (c + 1) * BANK], score[:], 1.0 / 128.0, neg_norm[:, kb : kb + 1],
+                    ALU.mult, ALU.add,
+                )
+
+            nc.scalar.activation(sig[:], adj[:], ACT.Sigmoid)
             codes_t_ps = psum_pre.tile([P, 2, K], BF16, name="codes_t_ps")
             for kb in range(KB):
                 for half in range(2):
                     nc.tensor.transpose(
                         codes_t_ps[:, half, kb * P : (kb + 1) * P], codes[:, kb, half * D : (half + 1) * D], ident_b[:]
                     )
-            codes_t = held.tile([P, 2, K], BF16, name="codes_t")
-            nc.scalar.copy(codes_t[:], codes_t_ps[:])
-            code_sq = held.tile([P, KB, 2 * D], F32, name="code_sq")
-            norm = held.tile([P, KB], F32, name="norm")
-            for kb in range(KB):
-                nc.scalar.activation(
-                    code_sq[:, kb, :], codes[:, kb, :], ACT.Square, scale=1.0 / 16.0, accum_out=norm[:, kb : kb + 1]
-                )
-
-            sq_r = held.tile([P, N], F32, name="sq_r")
-            sq_i = held.tile([P, N], F32, name="sq_i")
-            mag_sq = held.tile([P, N], F32, name="mag_sq")
-            mag = held.tile([P, N], F32, name="mag")
-            sum_sq = held.tile([P, 2], F32, name="sum_sq")
-            sum_mag = held.tile([P, 2], F32, name="sum_mag")
-            for h in range(2):
-                cols = slice(h * HALF, (h + 1) * HALF)
-                nc.gpsimd.tensor_tensor(sq_r[:, cols], zr[:, cols], zr[:, cols], ALU.mult)
-                nc.vector.tensor_tensor(sq_i[:, cols], zi[:, cols], zi[:, cols], ALU.mult)
-                nc.vector.scalar_tensor_tensor(
-                    mag_sq[:, cols], sq_r[:, cols], 1.0, sq_i[:, cols], ALU.mult, ALU.add, accum_out=sum_sq[:, h : h + 1]
-                )
-                nc.scalar.activation(mag[:, cols], mag_sq[:, cols], ACT.Sqrt, accum_out=sum_mag[:, h : h + 1])
-
-            for c in range(N // BANK):
-                cols = slice(c * BANK, (c + 1) * BANK)
-                for kb in range(KB):
-                    score = psum_pre.tile([P, BANK], F32, name="score", bufs=4)
-                    nc.tensor.matmul(score[:], codes_t[:, 0, kb * P : (kb + 1) * P], zr[:, cols], start=True, stop=False)
-                    nc.tensor.matmul(score[:], codes_t[:, 1, kb * P : (kb + 1) * P], zi[:, cols], start=False, stop=True)
-                    nc.vector.tensor_scalar(
-                        neg_dist[kb][:, cols], score[:], 1.0 / 128.0, norm[:, kb : kb + 1], ALU.mult, ALU.subtract
-                    )
+            squares(0)
+            nc.vector.tensor_copy(codes_t[:], codes_t_ps[:])
+            squares(1)
+            magnitudes(0)
+            score00 = scores(0, 0)
+            score01 = scores(0, 1)
+            code_norm(0)
+            magnitudes(1)
+            code_norm(1)
+            score10 = scores(1, 0)
+            negate_on_vector(0, 0, score00)
 
             mean_sq_ps = psum_pre.tile([P, 1], F32, name="mean_sq_ps")
             mean_mag_ps = psum_pre.tile([P, 1], F32, name="mean_mag_ps")
@@ -102,34 +127,36 @@ def tile_mirrorsystem_kernel(tc, z_real, z_imag, codebook, adj_t, offs, out):
             nc.vector.tensor_copy(mean_sq[:], mean_sq_ps[:])
             for h in range(2):
                 nc.tensor.matmul(mean_mag_ps[:], averager[:], sum_mag[:, h : h + 1], start=(h == 0), stop=(h == 1))
-            nc.vector.tensor_copy(mean_mag[:], mean_mag_ps[:])
+            score11 = scores(1, 1)
 
-        neg_var = held.tile([P, 1], F32, name="neg_var")
-        nc.vector.tensor_scalar(neg_var[:], mean_mag[:], mean_mag[:, 0:1], mean_sq[:, 0:1], ALU.mult, ALU.subtract)
-        nc.vector.tensor_scalar_mul(neg_var[:], neg_var[:], COUNT / (COUNT - 1.0))
-        exp_neg = held.tile([P, 1], F32, name="exp_neg")
-        nc.gpsimd.tensor_tensor(exp_neg[:], euler[:], neg_var[:], ALU.pow)
-        log_term = held.tile([P, 1], F32, name="log_term")
-        nc.scalar.activation(log_term[:], exp_neg[:], ACT.Ln, bias=1.0)
-        gam = held.tile([P, 1], F32, name="gam")
-        nc.vector.tensor_scalar(gam[:], log_term[:], neg_var[:, 0:1], 0.1, ALU.subtract, ALU.mult)
-
-        gate = [held.tile([P, K], F32, name=f"gate{kb}") for kb in range(KB)]
-        for kb in range(KB):
-            nc.vector.tensor_scalar_mul(gate[kb][:], sig[:, kb, :], gam[:, 0:1])
+            nc.vector.tensor_scalar(neg_var[:], mean_mag_ps[:], mean_mag_ps[:, 0:1], mean_sq[:, 0:1], ALU.mult, ALU.subtract)
+            nc.gpsimd.tensor_tensor(exp_neg[:], euler[:], neg_var[:], ALU.pow)
+            nc.vector.tensor_scalar_mul(tenth_var[:], neg_var[:], -0.1 * UNBIAS)
+            negate_on_vector(0, 1, score01)
+            negate_on_vector(1, 0, score10)
+            nc.scalar.activation(log_term[:], exp_neg[:], ACT.Ln, bias=1.0)
+            nc.vector.tensor_scalar(gam[0][:], log_term[:], 0.1, tenth_var[:, 0:1], ALU.mult, ALU.add)
+            nc.vector.tensor_scalar_mul(gate[0][:], sig[:, 0, :], gam[0][:, 0:1])
+            nc.scalar.activation(gam[1][:], log_term[:], ACT.Identity, bias=tenth_var[:, 0:1], scale=0.1)
+            nc.scalar.activation(gate[1][:], sig[:, 1, :], ACT.Copy, scale=gam[1][:, 0:1])
+            nc.scalar.activation(
+                neg_dist[1][:, BANK : 2 * BANK], score11[:], ACT.Identity, bias=neg_norm[:, 1:2], scale=1.0 / 128.0
+            )
 
         with (
-            tc.psum_pool(name="psum_t", bufs=2) as psum_t,
+            tc.psum_pool(name="psum_t", bufs=3) as psum_t,
             tc.psum_pool(name="psum_b", bufs=2) as psum_b,
             tc.psum_pool(name="psum_o", bufs=2) as psum_o,
         ):
             for c in range(N // PIECE):
-                cols = slice(c * PIECE, (c + 1) * PIECE)
                 piece_offsets = offsets[:, c * (PIECE // 16) : (c + 1) * (PIECE // 16)]
                 logits = [work.tile([P, PIECE], F32, name=f"logits{kb}") for kb in range(KB)]
                 for kb in range(KB):
                     nc.vector.tensor_tensor(
-                        logits[kb][:], gate[kb][:].indirect(piece_offsets), neg_dist[kb][:, cols], ALU.add
+                        logits[kb][:],
+                        gate[kb][:].indirect(piece_offsets),
+                        neg_dist[kb][:, c * PIECE : (c + 1) * PIECE],
+                        ALU.add,
                     )
                 logits_t = psum_t.tile([P, SUBS, K], F32, name="logits_t")
                 for s in range(SUBS):
@@ -139,28 +166,25 @@ def tile_mirrorsystem_kernel(tc, z_real, z_imag, codebook, adj_t, offs, out):
                         )
                 neg_max = small.tile([P, SUBS], F32, name="neg_max")
                 nc.vector.tensor_reduce(neg_max[:], logits_t[:], AX.X, ALU.max, negate=True)
-                expo = work.tile([P, SUBS, K], F32, name="expo")
-                denom = small.tile([P, SUBS], F32, name="denom")
                 for s in range(SUBS):
+                    expo = work.tile([P, K], F32, name="expo")
+                    denom = small.tile([P, 1], F32, name="denom")
                     nc.scalar.activation(
-                        expo[:, s, :], logits_t[:, s, :], ACT.Exp, bias=neg_max[:, s : s + 1], accum_out=denom[:, s : s + 1]
+                        expo[:], logits_t[:, s, :], ACT.Exp, bias=neg_max[:, s : s + 1], accum_out=denom[:]
                     )
-                recip = small.tile([P, SUBS], F32, name="recip")
-                nc.vector.reciprocal(recip[:], denom[:])
-                probs_t = work.tile([P, SUBS, K], BF16, name="probs_t")
-                for s in range(SUBS):
-                    nc.vector.tensor_scalar_mul(probs_t[:, s, :], expo[:, s, :], recip[:, s : s + 1])
-                probs_ps = psum_b.tile([P, KB, PIECE], BF16, name="probs_ps")
-                for kb in range(KB):
-                    for s in range(SUBS):
-                        nc.tensor.transpose(
-                            probs_ps[:, kb, s * P : (s + 1) * P], probs_t[:, s, kb * P : (kb + 1) * P], ident_b[:]
-                        )
-                probs = work.tile([P, KB, PIECE], BF16, name="probs")
-                nc.scalar.copy(probs[:], probs_ps[:])
-                quant_ps = psum_o.tile([P, PIECE], F32, name="quant_ps")
-                for kb in range(KB):
-                    nc.tensor.matmul(quant_ps[:], codes[:, kb, 0:D], probs[:, kb, :], start=(kb == 0), stop=(kb == KB - 1))
-                quant = work.tile([P, PIECE], F32, name="quant")
-                nc.scalar.copy(quant[:], quant_ps[:])
-                nc.sync.dma_start(out[:, cols], quant[:])
+                    recip = small.tile([P, 1], F32, name="recip")
+                    nc.vector.reciprocal(recip[:], denom[:])
+                    probs_t = work.tile([P, K], BF16, name="probs_t")
+                    nc.gpsimd.tensor_scalar(probs_t[:], expo[:], recip[:, 0:1], 1.0, ALU.mult, ALU.mult)
+                    probs_ps = psum_b.tile([P, KB, P], BF16, name="probs_ps")
+                    for kb in range(KB):
+                        nc.tensor.transpose(probs_ps[:, kb, :], probs_t[:, kb * P : (kb + 1) * P], ident_b[:])
+                    probs = work.tile([P, KB, P], BF16, name="probs")
+                    nc.scalar.copy(probs[:], probs_ps[:])
+                    quant_ps = psum_o.tile([P, P], F32, name="quant_ps")
+                    for kb in range(KB):
+                        nc.tensor.matmul(quant_ps[:], codes[:, kb, 0:D], probs[:, kb, :], start=(kb == 0), stop=(kb == KB - 1))
+                    quant = work.tile([P, P], F32, name="quant")
+                    nc.scalar.copy(quant[:], quant_ps[:])
+                    first = c * PIECE + s * P
+                    nc.sync.dma_start(out[:, first : first + P], quant[:])

@@ -114,11 +114,9 @@ def tile_mirrorsystem_kernel(tc, z_real, z_imag, codebook, adj_t, offs, out):
             magnitudes(0)
             score00 = scores(0, 0)
             score01 = scores(0, 1)
-            code_norm(0)
             magnitudes(1)
+            code_norm(0)
             code_norm(1)
-            score10 = scores(1, 0)
-            negate_on_vector(0, 0, score00)
 
             mean_sq_ps = psum_pre.tile([P, 1], F32, name="mean_sq_ps")
             mean_mag_ps = psum_pre.tile([P, 1], F32, name="mean_mag_ps")
@@ -127,21 +125,23 @@ def tile_mirrorsystem_kernel(tc, z_real, z_imag, codebook, adj_t, offs, out):
             nc.vector.tensor_copy(mean_sq[:], mean_sq_ps[:])
             for h in range(2):
                 nc.tensor.matmul(mean_mag_ps[:], averager[:], sum_mag[:, h : h + 1], start=(h == 0), stop=(h == 1))
+            score10 = scores(1, 0)
             score11 = scores(1, 1)
 
             nc.vector.tensor_scalar(neg_var[:], mean_mag_ps[:], mean_mag_ps[:, 0:1], mean_sq[:, 0:1], ALU.mult, ALU.subtract)
             nc.gpsimd.tensor_tensor(exp_neg[:], euler[:], neg_var[:], ALU.pow)
             nc.vector.tensor_scalar_mul(tenth_var[:], neg_var[:], -0.1 * UNBIAS)
+            negate_on_vector(0, 0, score00)
             negate_on_vector(0, 1, score01)
-            negate_on_vector(1, 0, score10)
             nc.scalar.activation(log_term[:], exp_neg[:], ACT.Ln, bias=1.0)
             nc.vector.tensor_scalar(gam[0][:], log_term[:], 0.1, tenth_var[:, 0:1], ALU.mult, ALU.add)
             nc.vector.tensor_scalar_mul(gate[0][:], sig[:, 0, :], gam[0][:, 0:1])
             nc.scalar.activation(gam[1][:], log_term[:], ACT.Identity, bias=tenth_var[:, 0:1], scale=0.1)
             nc.scalar.activation(gate[1][:], sig[:, 1, :], ACT.Copy, scale=gam[1][:, 0:1])
-            nc.scalar.activation(
-                neg_dist[1][:, BANK : 2 * BANK], score11[:], ACT.Identity, bias=neg_norm[:, 1:2], scale=1.0 / 128.0
-            )
+            for kb, score in enumerate((score10, score11)):
+                nc.scalar.activation(
+                    neg_dist[kb][:, BANK : 2 * BANK], score[:], ACT.Identity, bias=neg_norm[:, kb : kb + 1], scale=1.0 / 128.0
+                )
 
         with (
             tc.psum_pool(name="psum_t", bufs=3) as psum_t,
@@ -158,24 +158,19 @@ def tile_mirrorsystem_kernel(tc, z_real, z_imag, codebook, adj_t, offs, out):
                         neg_dist[kb][:, c * PIECE : (c + 1) * PIECE],
                         ALU.add,
                     )
-                logits_t = psum_t.tile([P, SUBS, K], F32, name="logits_t")
                 for s in range(SUBS):
+                    logits_t = psum_t.tile([P, K], F32, name="logits_t")
                     for kb in range(KB):
-                        nc.tensor.transpose(
-                            logits_t[:, s, kb * P : (kb + 1) * P], logits[kb][:, s * P : (s + 1) * P], ident_f[:]
-                        )
-                neg_max = small.tile([P, SUBS], F32, name="neg_max")
-                nc.vector.tensor_reduce(neg_max[:], logits_t[:], AX.X, ALU.max, negate=True)
-                for s in range(SUBS):
+                        nc.tensor.transpose(logits_t[:, kb * P : (kb + 1) * P], logits[kb][:, s * P : (s + 1) * P], ident_f[:])
+                    neg_max = small.tile([P, 1], F32, name="neg_max")
+                    nc.vector.tensor_reduce(neg_max[:], logits_t[:], AX.X, ALU.max, negate=True)
                     expo = work.tile([P, K], F32, name="expo")
                     denom = small.tile([P, 1], F32, name="denom")
-                    nc.scalar.activation(
-                        expo[:], logits_t[:, s, :], ACT.Exp, bias=neg_max[:, s : s + 1], accum_out=denom[:]
-                    )
+                    nc.scalar.activation(expo[:], logits_t[:], ACT.Exp, bias=neg_max[:, 0:1], accum_out=denom[:])
                     recip = small.tile([P, 1], F32, name="recip")
                     nc.vector.reciprocal(recip[:], denom[:])
                     probs_t = work.tile([P, K], BF16, name="probs_t")
-                    nc.gpsimd.tensor_scalar(probs_t[:], expo[:], recip[:, 0:1], 1.0, ALU.mult, ALU.mult)
+                    nc.vector.tensor_scalar_mul(probs_t[:], expo[:], recip[:, 0:1])
                     probs_ps = psum_b.tile([P, KB, P], BF16, name="probs_ps")
                     for kb in range(KB):
                         nc.tensor.transpose(probs_ps[:, kb, :], probs_t[:, kb * P : (kb + 1) * P], ident_b[:])

@@ -144,42 +144,48 @@ def tile_mirrorsystem_kernel(tc, z_real, z_imag, codebook, adj_t, offs, out):
                 )
 
         with (
-            tc.psum_pool(name="psum_t", bufs=3) as psum_t,
+            tc.psum_pool(name="psum_t", bufs=2) as psum_t,
             tc.psum_pool(name="psum_b", bufs=2) as psum_b,
             tc.psum_pool(name="psum_o", bufs=2) as psum_o,
         ):
             for c in range(N // PIECE):
+                cols = slice(c * PIECE, (c + 1) * PIECE)
                 piece_offsets = offsets[:, c * (PIECE // 16) : (c + 1) * (PIECE // 16)]
                 logits = [work.tile([P, PIECE], F32, name=f"logits{kb}") for kb in range(KB)]
                 for kb in range(KB):
                     nc.vector.tensor_tensor(
-                        logits[kb][:],
-                        gate[kb][:].indirect(piece_offsets),
-                        neg_dist[kb][:, c * PIECE : (c + 1) * PIECE],
-                        ALU.add,
+                        logits[kb][:], gate[kb][:].indirect(piece_offsets), neg_dist[kb][:, cols], ALU.add
                     )
+                logits_t = psum_t.tile([P, SUBS, K], F32, name="logits_t")
                 for s in range(SUBS):
-                    logits_t = psum_t.tile([P, K], F32, name="logits_t")
                     for kb in range(KB):
-                        nc.tensor.transpose(logits_t[:, kb * P : (kb + 1) * P], logits[kb][:, s * P : (s + 1) * P], ident_f[:])
-                    neg_max = small.tile([P, 1], F32, name="neg_max")
-                    nc.vector.tensor_reduce(neg_max[:], logits_t[:], AX.X, ALU.max, negate=True)
-                    expo = work.tile([P, K], F32, name="expo")
-                    denom = small.tile([P, 1], F32, name="denom")
-                    nc.scalar.activation(expo[:], logits_t[:], ACT.Exp, bias=neg_max[:, 0:1], accum_out=denom[:])
-                    recip = small.tile([P, 1], F32, name="recip")
-                    nc.vector.reciprocal(recip[:], denom[:])
-                    probs_t = work.tile([P, K], BF16, name="probs_t")
-                    nc.vector.tensor_scalar_mul(probs_t[:], expo[:], recip[:, 0:1])
-                    probs_ps = psum_b.tile([P, KB, P], BF16, name="probs_ps")
-                    for kb in range(KB):
-                        nc.tensor.transpose(probs_ps[:, kb, :], probs_t[:, kb * P : (kb + 1) * P], ident_b[:])
-                    probs = work.tile([P, KB, P], BF16, name="probs")
-                    nc.scalar.copy(probs[:], probs_ps[:])
-                    quant_ps = psum_o.tile([P, P], F32, name="quant_ps")
-                    for kb in range(KB):
-                        nc.tensor.matmul(quant_ps[:], codes[:, kb, 0:D], probs[:, kb, :], start=(kb == 0), stop=(kb == KB - 1))
-                    quant = work.tile([P, P], F32, name="quant")
-                    nc.scalar.copy(quant[:], quant_ps[:])
-                    first = c * PIECE + s * P
-                    nc.sync.dma_start(out[:, first : first + P], quant[:])
+                        nc.tensor.transpose(
+                            logits_t[:, s, kb * P : (kb + 1) * P], logits[kb][:, s * P : (s + 1) * P], ident_f[:]
+                        )
+                neg_max = small.tile([P, SUBS], F32, name="neg_max")
+                nc.vector.tensor_reduce(neg_max[:], logits_t[:], AX.X, ALU.max, negate=True)
+                expo = work.tile([P, SUBS, K], F32, name="expo")
+                denom = small.tile([P, SUBS], F32, name="denom")
+                for s in range(SUBS):
+                    nc.scalar.activation(
+                        expo[:, s, :], logits_t[:, s, :], ACT.Exp, bias=neg_max[:, s : s + 1], accum_out=denom[:, s : s + 1]
+                    )
+                recip = small.tile([P, SUBS], F32, name="recip")
+                nc.vector.reciprocal(recip[:], denom[:])
+                probs_t = work.tile([P, SUBS, K], BF16, name="probs_t")
+                for s in range(SUBS):
+                    nc.vector.tensor_scalar_mul(probs_t[:, s, :], expo[:, s, :], recip[:, s : s + 1])
+                probs_ps = psum_b.tile([P, KB, PIECE], BF16, name="probs_ps")
+                for kb in range(KB):
+                    for s in range(SUBS):
+                        nc.tensor.transpose(
+                            probs_ps[:, kb, s * P : (s + 1) * P], probs_t[:, s, kb * P : (kb + 1) * P], ident_b[:]
+                        )
+                probs = work.tile([P, KB, PIECE], BF16, name="probs")
+                nc.scalar.copy(probs[:], probs_ps[:])
+                quant_ps = psum_o.tile([P, PIECE], F32, name="quant_ps")
+                for kb in range(KB):
+                    nc.tensor.matmul(quant_ps[:], codes[:, kb, 0:D], probs[:, kb, :], start=(kb == 0), stop=(kb == KB - 1))
+                quant = work.tile([P, PIECE], F32, name="quant")
+                nc.scalar.copy(quant[:], quant_ps[:])
+                nc.sync.dma_start(out[:, cols], quant[:])

@@ -26,97 +26,74 @@ def tile_mirrorsystem_kernel(tc, z_real, z_imag, codebook, adj_t, offs, out):
     nc = tc.nc
     with (
         tc.tile_pool(name="held", bufs=1) as held,
-        tc.tile_pool(name="work", bufs=3) as work,
-        tc.tile_pool(name="small", bufs=4) as small,
+        tc.tile_pool(name="work", bufs=2) as work,
+        tc.tile_pool(name="small", bufs=2) as small,
     ):
         adj = held.tile([P, KB, K], F32, name="adj")
-        nc.sync.dma_start(adj[:], adj_t.rearrange("(b p) n -> p b n", p=P))
+        nc.scalar.dma_start(adj[:], adj_t.rearrange("(b p) n -> p b n", p=P))
         zr = held.tile([P, N], BF16, name="zr")
-        nc.scalar.dma_start(zr[:], z_real)
+        nc.sync.dma_start(zr[:], z_real)
         zi = held.tile([P, N], BF16, name="zi")
         nc.sync.dma_start(zi[:], z_imag)
-        codes = held.tile([P, KB, 2 * D], BF16, name="codes")
-        nc.scalar.dma_start(codes[:], codebook.rearrange("(b p) e -> p b e", p=P))
         offsets = held.tile([P, N // 16], U16, name="offsets")
         nc.sync.dma_start(offsets[:], offs)
+        codes = held.tile([P, KB, 2 * D], BF16, name="codes")
+        nc.scalar.dma_start(codes[:], codebook.rearrange("(b p) e -> p b e", p=P))
 
-        ident_b = held.tile([P, P], BF16, name="ident_b")
-        make_identity(nc, ident_b[:])
         ident_f = held.tile([P, P], F32, name="ident_f")
         make_identity(nc, ident_f[:])
+        ident_b = held.tile([P, P], BF16, name="ident_b")
+        make_identity(nc, ident_b[:])
         averager = held.tile([P, P], F32, name="averager")
         nc.vector.memset(averager[:], 1.0 / COUNT)
         euler = held.tile([P, 1], F32, name="euler")
         nc.vector.memset(euler[:], EULER**UNBIAS)
 
         sig = held.tile([P, KB, K], F32, name="sig")
-        codes_t = held.tile([P, 2, K], BF16, name="codes_t")
-        sq_r = held.tile([P, N], F32, name="sq_r")
-        sq_i = held.tile([P, N], F32, name="sq_i")
-        mag_sq = held.tile([P, N], F32, name="mag_sq")
-        mag = held.tile([P, N], F32, name="mag")
-        sum_sq = held.tile([P, 2], F32, name="sum_sq")
-        sum_mag = held.tile([P, 2], F32, name="sum_mag")
-        code_sq = held.tile([P, KB, 2 * D], F32, name="code_sq")
-        neg_norm = held.tile([P, KB], F32, name="neg_norm")
-        mean_sq = held.tile([P, 1], F32, name="mean_sq")
-        neg_var = held.tile([P, 1], F32, name="neg_var")
-        tenth_var = held.tile([P, 1], F32, name="tenth_var")
-        exp_neg = held.tile([P, 1], F32, name="exp_neg")
-        log_term = held.tile([P, 1], F32, name="log_term")
-        gam = [held.tile([P, 1], F32, name=f"gam{kb}") for kb in range(KB)]
+        nc.scalar.activation(sig[:], adj[:], ACT.Sigmoid)
+
         neg_dist = [held.tile([P, N], F32, name=f"neg_dist{kb}") for kb in range(KB)]
-        gate = [held.tile([P, K], F32, name=f"gate{kb}") for kb in range(KB)]
-
-        def squares(h):
-            cols = slice(h * HALF, (h + 1) * HALF)
-            nc.gpsimd.tensor_tensor(sq_r[:, cols], zr[:, cols], zr[:, cols], ALU.mult)
-            nc.vector.tensor_tensor(sq_i[:, cols], zi[:, cols], zi[:, cols], ALU.mult)
-
-        def magnitudes(h):
-            cols = slice(h * HALF, (h + 1) * HALF)
-            nc.vector.scalar_tensor_tensor(
-                mag_sq[:, cols], sq_r[:, cols], 1.0, sq_i[:, cols], ALU.mult, ALU.add, accum_out=sum_sq[:, h : h + 1]
-            )
-            nc.scalar.activation(mag[:, cols], mag_sq[:, cols], ACT.Sqrt, accum_out=sum_mag[:, h : h + 1])
-
-        def code_norm(kb):
-            nc.vector.scalar_tensor_tensor(
-                code_sq[:, kb, :], codes[:, kb, :], -1.0 / 256.0, codes[:, kb, :], ALU.mult, ALU.mult,
-                accum_out=neg_norm[:, kb : kb + 1],
-            )
-
+        mean_sq = held.tile([P, 1], F32, name="mean_sq")
         with tc.psum_pool(name="psum_pre", bufs=1) as psum_pre:
-
-            def scores(c, kb):
-                cols = slice(c * BANK, (c + 1) * BANK)
-                score = psum_pre.tile([P, BANK], F32, name="score", bufs=4)
-                nc.tensor.matmul(score[:], codes_t[:, 0, kb * P : (kb + 1) * P], zr[:, cols], start=True, stop=False)
-                nc.tensor.matmul(score[:], codes_t[:, 1, kb * P : (kb + 1) * P], zi[:, cols], start=False, stop=True)
-                return score
-
-            def negate_on_vector(c, kb, score):
-                nc.vector.tensor_scalar(
-                    neg_dist[kb][:, c * BANK : (c + 1) * BANK], score[:], 1.0 / 128.0, neg_norm[:, kb : kb + 1],
-                    ALU.mult, ALU.add,
-                )
-
-            nc.scalar.activation(sig[:], adj[:], ACT.Sigmoid)
             codes_t_ps = psum_pre.tile([P, 2, K], BF16, name="codes_t_ps")
             for kb in range(KB):
                 for half in range(2):
                     nc.tensor.transpose(
                         codes_t_ps[:, half, kb * P : (kb + 1) * P], codes[:, kb, half * D : (half + 1) * D], ident_b[:]
                     )
-            squares(0)
-            nc.vector.tensor_copy(codes_t[:], codes_t_ps[:])
-            squares(1)
-            magnitudes(0)
-            score00 = scores(0, 0)
-            score01 = scores(0, 1)
-            magnitudes(1)
-            code_norm(0)
-            code_norm(1)
+            codes_t = held.tile([P, 2, K], BF16, name="codes_t")
+            nc.scalar.copy(codes_t[:], codes_t_ps[:])
+            code_sq = held.tile([P, KB, 2 * D], F32, name="code_sq")
+            norm = held.tile([P, KB], F32, name="norm")
+            for kb in range(KB):
+                nc.scalar.activation(
+                    code_sq[:, kb, :], codes[:, kb, :], ACT.Square, scale=1.0 / 16.0, accum_out=norm[:, kb : kb + 1]
+                )
+
+            sq_r = held.tile([P, N], F32, name="sq_r")
+            sq_i = held.tile([P, N], F32, name="sq_i")
+            mag_sq = held.tile([P, N], F32, name="mag_sq")
+            mag = held.tile([P, N], F32, name="mag")
+            sum_sq = held.tile([P, 2], F32, name="sum_sq")
+            sum_mag = held.tile([P, 2], F32, name="sum_mag")
+            for h in range(2):
+                cols = slice(h * HALF, (h + 1) * HALF)
+                nc.gpsimd.tensor_tensor(sq_r[:, cols], zr[:, cols], zr[:, cols], ALU.mult)
+                nc.vector.tensor_tensor(sq_i[:, cols], zi[:, cols], zi[:, cols], ALU.mult)
+                nc.vector.scalar_tensor_tensor(
+                    mag_sq[:, cols], sq_r[:, cols], 1.0, sq_i[:, cols], ALU.mult, ALU.add, accum_out=sum_sq[:, h : h + 1]
+                )
+                nc.scalar.activation(mag[:, cols], mag_sq[:, cols], ACT.Sqrt, accum_out=sum_mag[:, h : h + 1])
+
+            for c in range(N // BANK):
+                cols = slice(c * BANK, (c + 1) * BANK)
+                for kb in range(KB):
+                    score = psum_pre.tile([P, BANK], F32, name="score", bufs=4)
+                    nc.tensor.matmul(score[:], codes_t[:, 0, kb * P : (kb + 1) * P], zr[:, cols], start=True, stop=False)
+                    nc.tensor.matmul(score[:], codes_t[:, 1, kb * P : (kb + 1) * P], zi[:, cols], start=False, stop=True)
+                    nc.vector.tensor_scalar(
+                        neg_dist[kb][:, cols], score[:], 1.0 / 128.0, norm[:, kb : kb + 1], ALU.mult, ALU.subtract
+                    )
 
             mean_sq_ps = psum_pre.tile([P, 1], F32, name="mean_sq_ps")
             mean_mag_ps = psum_pre.tile([P, 1], F32, name="mean_mag_ps")
@@ -125,23 +102,21 @@ def tile_mirrorsystem_kernel(tc, z_real, z_imag, codebook, adj_t, offs, out):
             nc.vector.tensor_copy(mean_sq[:], mean_sq_ps[:])
             for h in range(2):
                 nc.tensor.matmul(mean_mag_ps[:], averager[:], sum_mag[:, h : h + 1], start=(h == 0), stop=(h == 1))
-            score10 = scores(1, 0)
-            score11 = scores(1, 1)
-
+            neg_var = held.tile([P, 1], F32, name="neg_var")
             nc.vector.tensor_scalar(neg_var[:], mean_mag_ps[:], mean_mag_ps[:, 0:1], mean_sq[:, 0:1], ALU.mult, ALU.subtract)
-            nc.gpsimd.tensor_tensor(exp_neg[:], euler[:], neg_var[:], ALU.pow)
-            nc.vector.tensor_scalar_mul(tenth_var[:], neg_var[:], -0.1 * UNBIAS)
-            negate_on_vector(0, 0, score00)
-            negate_on_vector(0, 1, score01)
-            nc.scalar.activation(log_term[:], exp_neg[:], ACT.Ln, bias=1.0)
-            nc.vector.tensor_scalar(gam[0][:], log_term[:], 0.1, tenth_var[:, 0:1], ALU.mult, ALU.add)
-            nc.vector.tensor_scalar_mul(gate[0][:], sig[:, 0, :], gam[0][:, 0:1])
-            nc.scalar.activation(gam[1][:], log_term[:], ACT.Identity, bias=tenth_var[:, 0:1], scale=0.1)
-            nc.scalar.activation(gate[1][:], sig[:, 1, :], ACT.Copy, scale=gam[1][:, 0:1])
-            for kb, score in enumerate((score10, score11)):
-                nc.scalar.activation(
-                    neg_dist[kb][:, BANK : 2 * BANK], score[:], ACT.Identity, bias=neg_norm[:, kb : kb + 1], scale=1.0 / 128.0
-                )
+
+        exp_neg = held.tile([P, 1], F32, name="exp_neg")
+        nc.gpsimd.tensor_tensor(exp_neg[:], euler[:], neg_var[:], ALU.pow)
+        tenth_var = held.tile([P, 1], F32, name="tenth_var")
+        nc.vector.tensor_scalar_mul(tenth_var[:], neg_var[:], -0.1 * UNBIAS)
+        log_term = held.tile([P, 1], F32, name="log_term")
+        nc.scalar.activation(log_term[:], exp_neg[:], ACT.Ln, bias=1.0)
+        gam = held.tile([P, 1], F32, name="gam")
+        nc.vector.tensor_scalar(gam[:], log_term[:], 0.1, tenth_var[:, 0:1], ALU.mult, ALU.add)
+
+        gate = [held.tile([P, K], F32, name=f"gate{kb}") for kb in range(KB)]
+        for kb in range(KB):
+            nc.vector.tensor_scalar_mul(gate[kb][:], sig[:, kb, :], gam[:, 0:1])
 
         with (
             tc.psum_pool(name="psum_t", bufs=2) as psum_t,

@@ -32,9 +32,11 @@ def tile_mirrorsystem_kernel(tc, z_real, z_imag, codebook, adj_t, offs, out):
         adj = held.tile([P, KB, K], F32, name="adj")
         nc.scalar.dma_start(adj[:], adj_t.rearrange("(b p) n -> p b n", p=P))
         zr = held.tile([P, N], BF16, name="zr")
-        nc.sync.dma_start(zr[:], z_real)
         zi = held.tile([P, N], BF16, name="zi")
-        nc.sync.dma_start(zi[:], z_imag)
+        for h in range(2):
+            cols = slice(h * HALF, (h + 1) * HALF)
+            nc.sync.dma_start(zr[:, cols], z_real[:, cols])
+            nc.sync.dma_start(zi[:, cols], z_imag[:, cols])
         offsets = held.tile([P, N // 16], U16, name="offsets")
         nc.sync.dma_start(offsets[:], offs)
         codes = held.tile([P, KB, 2 * D], BF16, name="codes")
@@ -157,7 +159,7 @@ def tile_mirrorsystem_kernel(tc, z_real, z_imag, codebook, adj_t, offs, out):
                             probs_ps[:, kb, s * P : (s + 1) * P], probs_t[:, s, kb * P : (kb + 1) * P], ident_b[:]
                         )
                 probs = work.tile([P, KB, PIECE], BF16, name="probs")
-                nc.scalar.copy(probs[:], probs_ps[:])
+                nc.vector.tensor_copy(probs[:], probs_ps[:])
                 quant_ps = psum_o.tile([P, PIECE], F32, name="quant_ps")
                 for kb in range(KB):
                     nc.tensor.matmul(quant_ps[:], codes[:, kb, 0:D], probs[:, kb, :], start=(kb == 0), stop=(kb == KB - 1))

@@ -121,14 +121,15 @@ def tile_mirrorsystem_kernel(tc, z_real, z_imag, codebook, adj_t, offs, out):
             nc.vector.tensor_scalar_mul(gate[kb][:], sig[:, kb, :], gam[:, 0:1])
 
         with (
-            tc.psum_pool(name="psum_t", bufs=2) as psum_t,
+            tc.psum_pool(name="psum_t", bufs=N // PIECE) as psum_t,
             tc.psum_pool(name="psum_b", bufs=2) as psum_b,
             tc.psum_pool(name="psum_o", bufs=2) as psum_o,
         ):
+            transposed = []
             for c in range(N // PIECE):
                 cols = slice(c * PIECE, (c + 1) * PIECE)
                 piece_offsets = offsets[:, c * (PIECE // 16) : (c + 1) * (PIECE // 16)]
-                logits = [work.tile([P, PIECE], F32, name=f"logits{kb}") for kb in range(KB)]
+                logits = [work.tile([P, PIECE], F32, name=f"logits{kb}", bufs=N // PIECE) for kb in range(KB)]
                 for kb in range(KB):
                     nc.vector.tensor_tensor(
                         logits[kb][:], gate[kb][:].indirect(piece_offsets), neg_dist[kb][:, cols], ALU.add
@@ -139,6 +140,10 @@ def tile_mirrorsystem_kernel(tc, z_real, z_imag, codebook, adj_t, offs, out):
                         nc.tensor.transpose(
                             logits_t[:, s, kb * P : (kb + 1) * P], logits[kb][:, s * P : (s + 1) * P], ident_f[:]
                         )
+                transposed.append(logits_t)
+
+            for c, logits_t in enumerate(transposed):
+                cols = slice(c * PIECE, (c + 1) * PIECE)
                 neg_max = small.tile([P, SUBS], F32, name="neg_max")
                 nc.vector.tensor_reduce(neg_max[:], logits_t[:], AX.X, ALU.max, negate=True)
                 expo = work.tile([P, SUBS, K], F32, name="expo")

@@ -12,8 +12,8 @@ P = 128
 D, K, N = 128, 256, 1024
 KB = K // P
 PIECE = 256
+PIECES = N // PIECE
 SUBS = PIECE // P
-BANK = 512
 HALF = N // 2
 COUNT = D * N
 UNBIAS = COUNT / (COUNT - 1.0)
@@ -28,6 +28,9 @@ def tile_mirrorsystem_kernel(tc, z_real, z_imag, codebook, adj_t, offs, out):
         tc.tile_pool(name="held", bufs=1) as held,
         tc.tile_pool(name="work", bufs=2) as work,
         tc.tile_pool(name="small", bufs=2) as small,
+        tc.psum_pool(name="psum_wide", bufs=4) as psum_wide,
+        tc.psum_pool(name="psum_tiny", bufs=2) as psum_tiny,
+        tc.psum_pool(name="psum_last", bufs=2) as psum_last,
     ):
         adj = held.tile([P, KB, K], F32, name="adj")
         nc.scalar.dma_start(adj[:], adj_t.rearrange("(b p) n -> p b n", p=P))
@@ -50,62 +53,57 @@ def tile_mirrorsystem_kernel(tc, z_real, z_imag, codebook, adj_t, offs, out):
         nc.vector.memset(averager[:], 1.0 / COUNT)
         euler = held.tile([P, 1], F32, name="euler")
         nc.vector.memset(euler[:], EULER**UNBIAS)
+        ones_col = held.tile([P, 1], BF16, name="ones_col")
+        nc.vector.memset(ones_col[:], 1.0)
 
         sig = held.tile([P, KB, K], F32, name="sig")
         nc.scalar.activation(sig[:], adj[:], ACT.Sigmoid)
 
-        neg_dist = [held.tile([P, N], F32, name=f"neg_dist{kb}") for kb in range(KB)]
+        codes_t_ps = psum_wide.tile([P, 2, K], BF16, name="codes_t_ps", tag="wide")
+        for kb in range(KB):
+            for half in range(2):
+                nc.tensor.transpose(
+                    codes_t_ps[:, half, kb * P : (kb + 1) * P], codes[:, kb, half * D : (half + 1) * D], ident_b[:]
+                )
+        codes_t = held.tile([P, 2, K], BF16, name="codes_t")
+        nc.scalar.copy(codes_t[:], codes_t_ps[:])
+        code_sq = held.tile([P, KB, 2 * D], F32, name="code_sq")
+        norm = held.tile([P, KB], F32, name="norm")
+        for kb in range(KB):
+            nc.scalar.activation(
+                code_sq[:, kb, :], codes[:, kb, :], ACT.Square, scale=1.0 / 16.0, accum_out=norm[:, kb : kb + 1]
+            )
+        neg_norm = held.tile([P, KB], F32, name="neg_norm")
+        nc.vector.tensor_scalar_mul(neg_norm[:], norm[:], -1.0)
+        norm_hi = held.tile([P, KB], BF16, name="norm_hi")
+        nc.vector.tensor_scalar_mul(norm_hi[:], norm[:], -128.0)
+        norm_lo = held.tile([P, KB], BF16, name="norm_lo")
+        nc.vector.scalar_tensor_tensor(norm_lo[:], norm[:], -128.0, norm_hi[:], ALU.mult, ALU.subtract)
+
+        sq_r = held.tile([P, N], F32, name="sq_r")
+        sq_i = held.tile([P, N], F32, name="sq_i")
+        mag_sq = held.tile([P, N], F32, name="mag_sq")
+        mag = held.tile([P, N], F32, name="mag")
+        sum_sq = held.tile([P, 2], F32, name="sum_sq")
+        sum_mag = held.tile([P, 2], F32, name="sum_mag")
+        for h in range(2):
+            cols = slice(h * HALF, (h + 1) * HALF)
+            nc.gpsimd.tensor_tensor(sq_r[:, cols], zr[:, cols], zr[:, cols], ALU.mult)
+            nc.vector.tensor_tensor(sq_i[:, cols], zi[:, cols], zi[:, cols], ALU.mult)
+            nc.vector.scalar_tensor_tensor(
+                mag_sq[:, cols], sq_r[:, cols], 1.0, sq_i[:, cols], ALU.mult, ALU.add, accum_out=sum_sq[:, h : h + 1]
+            )
+            nc.scalar.activation(mag[:, cols], mag_sq[:, cols], ACT.Sqrt, accum_out=sum_mag[:, h : h + 1])
+
+        means_ps = psum_tiny.tile([P, 2], F32, name="means_ps", tag="tiny")
+        for h in range(2):
+            nc.tensor.matmul(means_ps[:, 0:1], averager[:], sum_sq[:, h : h + 1], start=(h == 0), stop=(h == 1))
         mean_sq = held.tile([P, 1], F32, name="mean_sq")
-        with tc.psum_pool(name="psum_pre", bufs=1) as psum_pre:
-            codes_t_ps = psum_pre.tile([P, 2, K], BF16, name="codes_t_ps")
-            for kb in range(KB):
-                for half in range(2):
-                    nc.tensor.transpose(
-                        codes_t_ps[:, half, kb * P : (kb + 1) * P], codes[:, kb, half * D : (half + 1) * D], ident_b[:]
-                    )
-            codes_t = held.tile([P, 2, K], BF16, name="codes_t")
-            nc.scalar.copy(codes_t[:], codes_t_ps[:])
-            code_sq = held.tile([P, KB, 2 * D], F32, name="code_sq")
-            norm = held.tile([P, KB], F32, name="norm")
-            for kb in range(KB):
-                nc.scalar.activation(
-                    code_sq[:, kb, :], codes[:, kb, :], ACT.Square, scale=1.0 / 16.0, accum_out=norm[:, kb : kb + 1]
-                )
-
-            sq_r = held.tile([P, N], F32, name="sq_r")
-            sq_i = held.tile([P, N], F32, name="sq_i")
-            mag_sq = held.tile([P, N], F32, name="mag_sq")
-            mag = held.tile([P, N], F32, name="mag")
-            sum_sq = held.tile([P, 2], F32, name="sum_sq")
-            sum_mag = held.tile([P, 2], F32, name="sum_mag")
-            for h in range(2):
-                cols = slice(h * HALF, (h + 1) * HALF)
-                nc.gpsimd.tensor_tensor(sq_r[:, cols], zr[:, cols], zr[:, cols], ALU.mult)
-                nc.vector.tensor_tensor(sq_i[:, cols], zi[:, cols], zi[:, cols], ALU.mult)
-                nc.vector.scalar_tensor_tensor(
-                    mag_sq[:, cols], sq_r[:, cols], 1.0, sq_i[:, cols], ALU.mult, ALU.add, accum_out=sum_sq[:, h : h + 1]
-                )
-                nc.scalar.activation(mag[:, cols], mag_sq[:, cols], ACT.Sqrt, accum_out=sum_mag[:, h : h + 1])
-
-            for c in range(N // BANK):
-                cols = slice(c * BANK, (c + 1) * BANK)
-                for kb in range(KB):
-                    score = psum_pre.tile([P, BANK], F32, name="score", bufs=4)
-                    nc.tensor.matmul(score[:], codes_t[:, 0, kb * P : (kb + 1) * P], zr[:, cols], start=True, stop=False)
-                    nc.tensor.matmul(score[:], codes_t[:, 1, kb * P : (kb + 1) * P], zi[:, cols], start=False, stop=True)
-                    nc.vector.tensor_scalar(
-                        neg_dist[kb][:, cols], score[:], 1.0 / 128.0, norm[:, kb : kb + 1], ALU.mult, ALU.subtract
-                    )
-
-            mean_sq_ps = psum_pre.tile([P, 1], F32, name="mean_sq_ps")
-            mean_mag_ps = psum_pre.tile([P, 1], F32, name="mean_mag_ps")
-            for h in range(2):
-                nc.tensor.matmul(mean_sq_ps[:], averager[:], sum_sq[:, h : h + 1], start=(h == 0), stop=(h == 1))
-            nc.vector.tensor_copy(mean_sq[:], mean_sq_ps[:])
-            for h in range(2):
-                nc.tensor.matmul(mean_mag_ps[:], averager[:], sum_mag[:, h : h + 1], start=(h == 0), stop=(h == 1))
-            neg_var = held.tile([P, 1], F32, name="neg_var")
-            nc.vector.tensor_scalar(neg_var[:], mean_mag_ps[:], mean_mag_ps[:, 0:1], mean_sq[:, 0:1], ALU.mult, ALU.subtract)
+        nc.vector.tensor_copy(mean_sq[:], means_ps[:, 0:1])
+        for h in range(2):
+            nc.tensor.matmul(means_ps[:, 1:2], averager[:], sum_mag[:, h : h + 1], start=(h == 0), stop=(h == 1))
+        neg_var = held.tile([P, 1], F32, name="neg_var")
+        nc.vector.tensor_scalar(neg_var[:], means_ps[:, 1:2], means_ps[:, 1:2], mean_sq[:, 0:1], ALU.mult, ALU.subtract)
 
         exp_neg = held.tile([P, 1], F32, name="exp_neg")
         nc.gpsimd.tensor_tensor(exp_neg[:], euler[:], neg_var[:], ALU.pow)
@@ -118,56 +116,78 @@ def tile_mirrorsystem_kernel(tc, z_real, z_imag, codebook, adj_t, offs, out):
 
         gate = [held.tile([P, K], F32, name=f"gate{kb}") for kb in range(KB)]
         for kb in range(KB):
-            nc.vector.tensor_scalar_mul(gate[kb][:], sig[:, kb, :], gam[:, 0:1])
+            nc.vector.tensor_scalar(gate[kb][:], sig[:, kb, :], 1.0, gam[:, 0:1], ALU.subtract, ALU.mult)
 
-        with (
-            tc.psum_pool(name="psum_t", bufs=N // PIECE) as psum_t,
-            tc.psum_pool(name="psum_b", bufs=2) as psum_b,
-            tc.psum_pool(name="psum_o", bufs=2) as psum_o,
-        ):
-            transposed = []
-            for c in range(N // PIECE):
-                cols = slice(c * PIECE, (c + 1) * PIECE)
-                piece_offsets = offsets[:, c * (PIECE // 16) : (c + 1) * (PIECE // 16)]
-                logits = [work.tile([P, PIECE], F32, name=f"logits{kb}", bufs=N // PIECE) for kb in range(KB)]
+        shift_hi = held.tile([P, N // P], BF16, name="shift_hi")
+        shift_lo = held.tile([P, N // P], BF16, name="shift_lo")
+        for c in range(PIECES):
+            blocks = slice(c * SUBS, (c + 1) * SUBS)
+            score_t = psum_wide.tile([P, SUBS, K], F32, name="score_t", tag="wide")
+            for s in range(SUBS):
+                tokens = slice((c * SUBS + s) * P, (c * SUBS + s + 1) * P)
+                nc.tensor.matmul(score_t[:, s, :], zr[:, tokens], codes_t[:, 0, :], start=True, stop=False)
+                nc.tensor.matmul(score_t[:, s, :], zi[:, tokens], codes_t[:, 1, :], start=False, stop=False)
                 for kb in range(KB):
-                    nc.vector.tensor_tensor(
-                        logits[kb][:], gate[kb][:].indirect(piece_offsets), neg_dist[kb][:, cols], ALU.add
+                    symbols = slice(kb * P, (kb + 1) * P)
+                    nc.tensor.matmul(
+                        score_t[:, s, symbols], norm_hi[:, kb : kb + 1].to_broadcast([P, P]), ident_b[:], start=False, stop=False
                     )
-                logits_t = psum_t.tile([P, SUBS, K], F32, name="logits_t")
-                for s in range(SUBS):
-                    for kb in range(KB):
-                        nc.tensor.transpose(
-                            logits_t[:, s, kb * P : (kb + 1) * P], logits[kb][:, s * P : (s + 1) * P], ident_f[:]
-                        )
-                transposed.append(logits_t)
+                    nc.tensor.matmul(
+                        score_t[:, s, symbols], norm_lo[:, kb : kb + 1].to_broadcast([P, P]), ident_b[:],
+                        start=False, stop=(kb == KB - 1),
+                    )
+            top = small.tile([P, SUBS], F32, name="top")
+            nc.vector.tensor_reduce(top[:], score_t[:], AX.X, ALU.max)
+            nc.vector.tensor_scalar_mul(shift_hi[:, blocks], top[:], -1.0)
+            nc.vector.scalar_tensor_tensor(shift_lo[:, blocks], top[:], -1.0, shift_hi[:, blocks], ALU.mult, ALU.subtract)
 
-            for c, logits_t in enumerate(transposed):
-                cols = slice(c * PIECE, (c + 1) * PIECE)
-                neg_max = small.tile([P, SUBS], F32, name="neg_max")
-                nc.vector.tensor_reduce(neg_max[:], logits_t[:], AX.X, ALU.max, negate=True)
-                expo = work.tile([P, SUBS, K], F32, name="expo")
-                denom = small.tile([P, SUBS], F32, name="denom")
+        neg_dist = [held.tile([P, N], F32, name=f"neg_dist{kb}") for kb in range(KB)]
+        for c in range(PIECES):
+            cols = slice(c * PIECE, (c + 1) * PIECE)
+            score = psum_wide.tile([P, KB, PIECE], F32, name="score", tag="wide")
+            for kb in range(KB):
+                symbols = slice(kb * P, (kb + 1) * P)
+                nc.tensor.matmul(score[:, kb, :], codes_t[:, 0, symbols], zr[:, cols], start=True, stop=False)
+                nc.tensor.matmul(score[:, kb, :], codes_t[:, 1, symbols], zi[:, cols], start=False, stop=False)
                 for s in range(SUBS):
-                    nc.scalar.activation(
-                        expo[:, s, :], logits_t[:, s, :], ACT.Exp, bias=neg_max[:, s : s + 1], accum_out=denom[:, s : s + 1]
+                    b = c * SUBS + s
+                    tokens = slice(s * P, (s + 1) * P)
+                    nc.tensor.matmul(
+                        score[:, kb, tokens], shift_hi[:, b : b + 1].to_broadcast([P, P]), ident_b[:], start=False, stop=False
                     )
-                recip = small.tile([P, SUBS], F32, name="recip")
-                nc.vector.reciprocal(recip[:], denom[:])
-                probs_t = work.tile([P, SUBS, K], BF16, name="probs_t")
-                for s in range(SUBS):
-                    nc.vector.tensor_scalar_mul(probs_t[:, s, :], expo[:, s, :], recip[:, s : s + 1])
-                probs_ps = psum_b.tile([P, KB, PIECE], BF16, name="probs_ps")
+                    nc.tensor.matmul(
+                        score[:, kb, tokens], shift_lo[:, b : b + 1].to_broadcast([P, P]), ident_b[:],
+                        start=False, stop=(s == SUBS - 1),
+                    )
+                nc.scalar.activation(
+                    neg_dist[kb][:, cols], score[:, kb, :], ACT.Identity, scale=1.0 / 128.0, bias=neg_norm[:, kb : kb + 1]
+                )
+
+        for c in range(PIECES):
+            cols = slice(c * PIECE, (c + 1) * PIECE)
+            piece_offsets = offsets[:, c * (PIECE // 16) : (c + 1) * (PIECE // 16)]
+            expo = [work.tile([P, PIECE], BF16, name=f"expo{kb}") for kb in range(KB)]
+            for kb in range(KB):
+                logits = work.tile([P, PIECE], F32, name="logits")
+                nc.vector.tensor_tensor(logits[:], gate[kb][:].indirect(piece_offsets), neg_dist[kb][:, cols], ALU.add)
+                nc.scalar.activation(expo[kb][:], logits[:], ACT.Exp)
+            last = psum_last.tile([P, 2, PIECE], F32, name="last")
+            for kb in range(KB):
+                nc.tensor.matmul(last[:, 0, :], codes[:, kb, 0:D], expo[kb][:], start=(kb == 0), stop=(kb == KB - 1))
+            denom = psum_tiny.tile([P, SUBS], F32, name="denom", tag="tiny")
+            for s in range(SUBS):
                 for kb in range(KB):
-                    for s in range(SUBS):
-                        nc.tensor.transpose(
-                            probs_ps[:, kb, s * P : (s + 1) * P], probs_t[:, s, kb * P : (kb + 1) * P], ident_b[:]
-                        )
-                probs = work.tile([P, KB, PIECE], BF16, name="probs")
-                nc.vector.tensor_copy(probs[:], probs_ps[:])
-                quant_ps = psum_o.tile([P, PIECE], F32, name="quant_ps")
-                for kb in range(KB):
-                    nc.tensor.matmul(quant_ps[:], codes[:, kb, 0:D], probs[:, kb, :], start=(kb == 0), stop=(kb == KB - 1))
-                quant = work.tile([P, PIECE], F32, name="quant")
-                nc.scalar.copy(quant[:], quant_ps[:])
-                nc.sync.dma_start(out[:, cols], quant[:])
+                    nc.tensor.matmul(
+                        denom[:, s : s + 1], expo[kb][:, s * P : (s + 1) * P], ones_col[:], start=(kb == 0), stop=(kb == KB - 1)
+                    )
+            recip = small.tile([P, SUBS], F32, name="recip")
+            nc.vector.reciprocal(recip[:], denom[:])
+            quant = work.tile([P, PIECE], F32, name="quant")
+            nc.scalar.copy(quant[:], last[:, 0, :])
+            for s in range(SUBS):
+                nc.tensor.matmul(
+                    last[:, 1, s * P : (s + 1) * P], recip[:, s : s + 1].to_broadcast([P, P]), ident_f[:], start=True, stop=True
+                )
+            result = work.tile([P, PIECE], F32, name="result")
+            nc.vector.tensor_tensor(result[:], quant[:], last[:, 1, :], ALU.mult)
+            nc.sync.dma_start(out[:, cols], result[:])

@@ -14,6 +14,7 @@ KB = K // P
 PIECE = 256
 PIECES = N // PIECE
 SUBS = PIECE // P
+BANK = 512
 HALF = N // 2
 COUNT = D * N
 UNBIAS = COUNT / (COUNT - 1.0)
@@ -28,12 +29,12 @@ def tile_mirrorsystem_kernel(tc, z_real, z_imag, codebook, adj_t, offs, out):
         tc.tile_pool(name="held", bufs=1) as held,
         tc.tile_pool(name="work", bufs=2) as work,
         tc.tile_pool(name="small", bufs=2) as small,
-        tc.psum_pool(name="psum_wide", bufs=4) as psum_wide,
-        tc.psum_pool(name="psum_tiny", bufs=2) as psum_tiny,
-        tc.psum_pool(name="psum_last", bufs=2) as psum_last,
+        tc.psum_pool(name="psum_score", bufs=4) as psum_score,
     ):
         adj = held.tile([P, KB, K], F32, name="adj")
         nc.scalar.dma_start(adj[:], adj_t.rearrange("(b p) n -> p b n", p=P))
+        codes = held.tile([P, KB, 2 * D], BF16, name="codes")
+        nc.sync.dma_start(codes[:], codebook.rearrange("(b p) e -> p b e", p=P))
         zr = held.tile([P, N], BF16, name="zr")
         zi = held.tile([P, N], BF16, name="zi")
         for h in range(2):
@@ -42,152 +43,163 @@ def tile_mirrorsystem_kernel(tc, z_real, z_imag, codebook, adj_t, offs, out):
             nc.sync.dma_start(zi[:, cols], z_imag[:, cols])
         offsets = held.tile([P, N // 16], U16, name="offsets")
         nc.sync.dma_start(offsets[:], offs)
-        codes = held.tile([P, KB, 2 * D], BF16, name="codes")
-        nc.scalar.dma_start(codes[:], codebook.rearrange("(b p) e -> p b e", p=P))
 
-        ident_f = held.tile([P, P], F32, name="ident_f")
-        make_identity(nc, ident_f[:])
-        ident_b = held.tile([P, P], BF16, name="ident_b")
-        make_identity(nc, ident_b[:])
-        averager = held.tile([P, P], F32, name="averager")
-        nc.vector.memset(averager[:], 1.0 / COUNT)
         euler = held.tile([P, 1], F32, name="euler")
         nc.vector.memset(euler[:], EULER**UNBIAS)
+        averager = held.tile([P, P], F32, name="averager")
+        nc.vector.memset(averager[:], 1.0 / COUNT)
         ones_col = held.tile([P, 1], BF16, name="ones_col")
         nc.vector.memset(ones_col[:], 1.0)
+        ident_b = held.tile([P, P], BF16, name="ident_b")
+        make_identity(nc, ident_b[:])
+        ident_f = held.tile([P, P], F32, name="ident_f")
+        make_identity(nc, ident_f[:])
 
-        sig = held.tile([P, KB, K], F32, name="sig")
-        nc.scalar.activation(sig[:], adj[:], ACT.Sigmoid)
-
-        codes_t_ps = psum_wide.tile([P, 2, K], BF16, name="codes_t_ps", tag="wide")
-        for kb in range(KB):
-            for half in range(2):
-                nc.tensor.transpose(
-                    codes_t_ps[:, half, kb * P : (kb + 1) * P], codes[:, kb, half * D : (half + 1) * D], ident_b[:]
-                )
-        codes_t = held.tile([P, 2, K], BF16, name="codes_t")
-        nc.scalar.copy(codes_t[:], codes_t_ps[:])
-        code_sq = held.tile([P, KB, 2 * D], F32, name="code_sq")
-        norm = held.tile([P, KB], F32, name="norm")
-        for kb in range(KB):
-            nc.scalar.activation(
-                code_sq[:, kb, :], codes[:, kb, :], ACT.Square, scale=1.0 / 16.0, accum_out=norm[:, kb : kb + 1]
-            )
-        neg_norm = held.tile([P, KB], F32, name="neg_norm")
-        nc.vector.tensor_scalar_mul(neg_norm[:], norm[:], -1.0)
-        norm_hi = held.tile([P, KB], BF16, name="norm_hi")
-        nc.vector.tensor_scalar_mul(norm_hi[:], norm[:], -128.0)
-        norm_lo = held.tile([P, KB], BF16, name="norm_lo")
-        nc.vector.scalar_tensor_tensor(norm_lo[:], norm[:], -128.0, norm_hi[:], ALU.mult, ALU.subtract)
-
-        sq_r = held.tile([P, N], F32, name="sq_r")
-        sq_i = held.tile([P, N], F32, name="sq_i")
-        mag_sq = held.tile([P, N], F32, name="mag_sq")
-        mag = held.tile([P, N], F32, name="mag")
-        sum_sq = held.tile([P, 2], F32, name="sum_sq")
-        sum_mag = held.tile([P, 2], F32, name="sum_mag")
-        for h in range(2):
-            cols = slice(h * HALF, (h + 1) * HALF)
-            nc.gpsimd.tensor_tensor(sq_r[:, cols], zr[:, cols], zr[:, cols], ALU.mult)
-            nc.vector.tensor_tensor(sq_i[:, cols], zi[:, cols], zi[:, cols], ALU.mult)
-            nc.vector.scalar_tensor_tensor(
-                mag_sq[:, cols], sq_r[:, cols], 1.0, sq_i[:, cols], ALU.mult, ALU.add, accum_out=sum_sq[:, h : h + 1]
-            )
-            nc.scalar.activation(mag[:, cols], mag_sq[:, cols], ACT.Sqrt, accum_out=sum_mag[:, h : h + 1])
-
-        means_ps = psum_tiny.tile([P, 2], F32, name="means_ps", tag="tiny")
-        for h in range(2):
-            nc.tensor.matmul(means_ps[:, 0:1], averager[:], sum_sq[:, h : h + 1], start=(h == 0), stop=(h == 1))
-        mean_sq = held.tile([P, 1], F32, name="mean_sq")
-        nc.vector.tensor_copy(mean_sq[:], means_ps[:, 0:1])
-        for h in range(2):
-            nc.tensor.matmul(means_ps[:, 1:2], averager[:], sum_mag[:, h : h + 1], start=(h == 0), stop=(h == 1))
-        neg_var = held.tile([P, 1], F32, name="neg_var")
-        nc.vector.tensor_scalar(neg_var[:], means_ps[:, 1:2], means_ps[:, 1:2], mean_sq[:, 0:1], ALU.mult, ALU.subtract)
-
-        exp_neg = held.tile([P, 1], F32, name="exp_neg")
-        nc.gpsimd.tensor_tensor(exp_neg[:], euler[:], neg_var[:], ALU.pow)
-        tenth_var = held.tile([P, 1], F32, name="tenth_var")
-        nc.vector.tensor_scalar_mul(tenth_var[:], neg_var[:], -0.1 * UNBIAS)
-        log_term = held.tile([P, 1], F32, name="log_term")
-        nc.scalar.activation(log_term[:], exp_neg[:], ACT.Ln, bias=1.0)
-        gam = held.tile([P, 1], F32, name="gam")
-        nc.vector.tensor_scalar(gam[:], log_term[:], 0.1, tenth_var[:, 0:1], ALU.mult, ALU.add)
-
-        gate = [held.tile([P, K], F32, name=f"gate{kb}") for kb in range(KB)]
-        for kb in range(KB):
-            nc.vector.tensor_scalar(gate[kb][:], sig[:, kb, :], 1.0, gam[:, 0:1], ALU.subtract, ALU.mult)
-
-        shift_hi = held.tile([P, N // P], BF16, name="shift_hi")
-        shift_lo = held.tile([P, N // P], BF16, name="shift_lo")
-        for c in range(PIECES):
-            blocks = slice(c * SUBS, (c + 1) * SUBS)
-            score_t = psum_wide.tile([P, SUBS, K], F32, name="score_t", tag="wide")
-            for s in range(SUBS):
-                tokens = slice((c * SUBS + s) * P, (c * SUBS + s + 1) * P)
-                nc.tensor.matmul(score_t[:, s, :], zr[:, tokens], codes_t[:, 0, :], start=True, stop=False)
-                nc.tensor.matmul(score_t[:, s, :], zi[:, tokens], codes_t[:, 1, :], start=False, stop=False)
-                for kb in range(KB):
-                    symbols = slice(kb * P, (kb + 1) * P)
-                    nc.tensor.matmul(
-                        score_t[:, s, symbols], norm_hi[:, kb : kb + 1].to_broadcast([P, P]), ident_b[:], start=False, stop=False
-                    )
-                    nc.tensor.matmul(
-                        score_t[:, s, symbols], norm_lo[:, kb : kb + 1].to_broadcast([P, P]), ident_b[:],
-                        start=False, stop=(kb == KB - 1),
-                    )
-            top = small.tile([P, SUBS], F32, name="top")
-            nc.vector.tensor_reduce(top[:], score_t[:], AX.X, ALU.max)
-            nc.vector.tensor_scalar_mul(shift_hi[:, blocks], top[:], -1.0)
-            nc.vector.scalar_tensor_tensor(shift_lo[:, blocks], top[:], -1.0, shift_hi[:, blocks], ALU.mult, ALU.subtract)
+        warm = held.tile([P, 4], F32, name="warm")
+        nc.scalar.activation(warm[:, 0:1], euler[:], ACT.Sigmoid)
 
         neg_dist = [held.tile([P, N], F32, name=f"neg_dist{kb}") for kb in range(KB)]
-        for c in range(PIECES):
-            cols = slice(c * PIECE, (c + 1) * PIECE)
-            score = psum_wide.tile([P, KB, PIECE], F32, name="score", tag="wide")
+        neg_var = held.tile([P, 1], F32, name="neg_var")
+        shift_hi = held.tile([P, N // P], BF16, name="shift_hi")
+        shift_lo = held.tile([P, N // P], BF16, name="shift_lo")
+        with tc.psum_pool(name="psum_pre", bufs=1) as psum_pre:
+            code_sq = held.tile([P, KB, 2 * D], F32, name="code_sq")
+            norm = held.tile([P, KB], F32, name="norm")
             for kb in range(KB):
-                symbols = slice(kb * P, (kb + 1) * P)
-                nc.tensor.matmul(score[:, kb, :], codes_t[:, 0, symbols], zr[:, cols], start=True, stop=False)
-                nc.tensor.matmul(score[:, kb, :], codes_t[:, 1, symbols], zi[:, cols], start=False, stop=False)
-                for s in range(SUBS):
-                    b = c * SUBS + s
-                    tokens = slice(s * P, (s + 1) * P)
-                    nc.tensor.matmul(
-                        score[:, kb, tokens], shift_hi[:, b : b + 1].to_broadcast([P, P]), ident_b[:], start=False, stop=False
-                    )
-                    nc.tensor.matmul(
-                        score[:, kb, tokens], shift_lo[:, b : b + 1].to_broadcast([P, P]), ident_b[:],
-                        start=False, stop=(s == SUBS - 1),
-                    )
                 nc.scalar.activation(
-                    neg_dist[kb][:, cols], score[:, kb, :], ACT.Identity, scale=1.0 / 128.0, bias=neg_norm[:, kb : kb + 1]
+                    code_sq[:, kb, :], codes[:, kb, :], ACT.Square, scale=1.0 / 16.0, accum_out=norm[:, kb : kb + 1]
                 )
-
-        for c in range(PIECES):
-            cols = slice(c * PIECE, (c + 1) * PIECE)
-            piece_offsets = offsets[:, c * (PIECE // 16) : (c + 1) * (PIECE // 16)]
-            expo = [work.tile([P, PIECE], BF16, name=f"expo{kb}") for kb in range(KB)]
+            codes_t_ps = psum_pre.tile([P, 2, K], BF16, name="codes_t_ps", tag="wide", bufs=3)
             for kb in range(KB):
-                logits = work.tile([P, PIECE], F32, name="logits")
-                nc.vector.tensor_tensor(logits[:], gate[kb][:].indirect(piece_offsets), neg_dist[kb][:, cols], ALU.add)
-                nc.scalar.activation(expo[kb][:], logits[:], ACT.Exp)
-            last = psum_last.tile([P, 2, PIECE], F32, name="last")
-            for kb in range(KB):
-                nc.tensor.matmul(last[:, 0, :], codes[:, kb, 0:D], expo[kb][:], start=(kb == 0), stop=(kb == KB - 1))
-            denom = psum_tiny.tile([P, SUBS], F32, name="denom", tag="tiny")
-            for s in range(SUBS):
-                for kb in range(KB):
-                    nc.tensor.matmul(
-                        denom[:, s : s + 1], expo[kb][:, s * P : (s + 1) * P], ones_col[:], start=(kb == 0), stop=(kb == KB - 1)
+                for half in range(2):
+                    nc.tensor.transpose(
+                        codes_t_ps[:, half, kb * P : (kb + 1) * P], codes[:, kb, half * D : (half + 1) * D], ident_b[:]
                     )
-            recip = small.tile([P, SUBS], F32, name="recip")
-            nc.vector.reciprocal(recip[:], denom[:])
-            quant = work.tile([P, PIECE], F32, name="quant")
-            nc.scalar.copy(quant[:], last[:, 0, :])
-            for s in range(SUBS):
-                nc.tensor.matmul(
-                    last[:, 1, s * P : (s + 1) * P], recip[:, s : s + 1].to_broadcast([P, P]), ident_f[:], start=True, stop=True
+            codes_t = held.tile([P, 2, K], BF16, name="codes_t")
+            nc.vector.tensor_copy(codes_t[:], codes_t_ps[:])
+            neg_norm = held.tile([P, KB], F32, name="neg_norm")
+            nc.vector.tensor_scalar_mul(neg_norm[:], norm[:], -1.0)
+            norm_hi = held.tile([P, KB], BF16, name="norm_hi")
+            nc.vector.tensor_scalar_mul(norm_hi[:], norm[:], -128.0)
+            norm_lo = held.tile([P, KB], BF16, name="norm_lo")
+            nc.vector.scalar_tensor_tensor(norm_lo[:], norm[:], -128.0, norm_hi[:], ALU.mult, ALU.subtract)
+
+            sig = held.tile([P, KB, K], F32, name="sig")
+            nc.scalar.activation(sig[:], adj[:], ACT.Sigmoid)
+            nc.scalar.activation(warm[:, 1:2], sig[:, 0, 0:1], ACT.Sqrt)
+
+            sq_r = held.tile([P, N], F32, name="sq_r")
+            sq_i = held.tile([P, N], F32, name="sq_i")
+            mag_sq = held.tile([P, N], F32, name="mag_sq")
+            mag = held.tile([P, N], F32, name="mag")
+            sums = [held.tile([P, 2], F32, name=f"sums{h}") for h in range(2)]
+            means_ps = psum_pre.tile([P, 2], F32, name="means_ps")
+            for h in range(2):
+                cols = slice(h * HALF, (h + 1) * HALF)
+                nc.gpsimd.tensor_tensor(sq_r[:, cols], zr[:, cols], zr[:, cols], ALU.mult)
+                nc.vector.tensor_tensor(sq_i[:, cols], zi[:, cols], zi[:, cols], ALU.mult)
+            for h in range(2):
+                cols = slice(h * HALF, (h + 1) * HALF)
+                nc.vector.scalar_tensor_tensor(
+                    mag_sq[:, cols], sq_r[:, cols], 1.0, sq_i[:, cols], ALU.mult, ALU.add, accum_out=sums[h][:, 0:1]
                 )
-            result = work.tile([P, PIECE], F32, name="result")
-            nc.vector.tensor_tensor(result[:], quant[:], last[:, 1, :], ALU.mult)
-            nc.sync.dma_start(out[:, cols], result[:])
+                nc.scalar.activation(mag[:, cols], mag_sq[:, cols], ACT.Sqrt, accum_out=sums[h][:, 1:2])
+                nc.tensor.matmul(means_ps[:], averager[:], sums[h][:], start=(h == 0), stop=(h == 1))
+            nc.scalar.activation(warm[:, 2:3], sums[1][:, 1:2], ACT.Ln, bias=sums[0][:, 1:2])
+            nc.vector.tensor_scalar(neg_var[:], means_ps[:, 1:2], means_ps[:, 1:2], means_ps[:, 0:1], ALU.mult, ALU.subtract)
+
+            exp_neg = held.tile([P, 1], F32, name="exp_neg")
+            nc.gpsimd.tensor_tensor(exp_neg[:], euler[:], neg_var[:], ALU.pow)
+            tenth_var = held.tile([P, 1], F32, name="tenth_var")
+            nc.vector.tensor_scalar_mul(tenth_var[:], neg_var[:], -0.1 * UNBIAS)
+            log_term = held.tile([P, 1], F32, name="log_term")
+            nc.scalar.activation(log_term[:], exp_neg[:], ACT.Ln, bias=1.0)
+            nc.scalar.activation(warm[:, 3:4], log_term[:], ACT.Exp)
+            gam = held.tile([P, 1], F32, name="gam")
+            nc.vector.tensor_scalar(gam[:], log_term[:], 0.1, tenth_var[:, 0:1], ALU.mult, ALU.add)
+            gate = [held.tile([P, K], F32, name=f"gate{kb}") for kb in range(KB)]
+            for kb in range(KB):
+                nc.vector.tensor_scalar(gate[kb][:], sig[:, kb, :], 1.0, gam[:, 0:1], ALU.subtract, ALU.mult)
+
+            for c in range(PIECES):
+                blocks = slice(c * SUBS, (c + 1) * SUBS)
+                score_t = psum_pre.tile([P, SUBS, K], F32, name="score_t", tag="wide", bufs=3)
+                for s in range(SUBS):
+                    tokens = slice((c * SUBS + s) * P, (c * SUBS + s + 1) * P)
+                    nc.tensor.matmul(score_t[:, s, :], zr[:, tokens], codes_t[:, 0, :], start=True, stop=False)
+                    nc.tensor.matmul(score_t[:, s, :], zi[:, tokens], codes_t[:, 1, :], start=False, stop=False)
+                    for kb in range(KB):
+                        symbols = slice(kb * P, (kb + 1) * P)
+                        nc.tensor.matmul(
+                            score_t[:, s, symbols], norm_hi[:, kb : kb + 1].to_broadcast([P, P]), ident_b[:],
+                            start=False, stop=False,
+                        )
+                        nc.tensor.matmul(
+                            score_t[:, s, symbols], norm_lo[:, kb : kb + 1].to_broadcast([P, P]), ident_b[:],
+                            start=False, stop=(kb == KB - 1),
+                        )
+                top = small.tile([P, SUBS], F32, name="top")
+                nc.vector.tensor_reduce(top[:], score_t[:], AX.X, ALU.max)
+                nc.vector.tensor_scalar_mul(shift_hi[:, blocks], top[:], -1.0)
+                nc.vector.scalar_tensor_tensor(shift_lo[:, blocks], top[:], -1.0, shift_hi[:, blocks], ALU.mult, ALU.subtract)
+
+            for c in range(N // BANK):
+                cols = slice(c * BANK, (c + 1) * BANK)
+                for kb in range(KB):
+                    symbols = slice(kb * P, (kb + 1) * P)
+                    score = psum_score.tile([P, BANK], F32, name="score")
+                    nc.tensor.matmul(score[:], codes_t[:, 0, symbols], zr[:, cols], start=True, stop=False)
+                    nc.tensor.matmul(score[:], codes_t[:, 1, symbols], zi[:, cols], start=False, stop=False)
+                    for s in range(BANK // P):
+                        b = c * (BANK // P) + s
+                        tokens = slice(s * P, (s + 1) * P)
+                        nc.tensor.matmul(
+                            score[:, tokens], shift_hi[:, b : b + 1].to_broadcast([P, P]), ident_b[:], start=False, stop=False
+                        )
+                        nc.tensor.matmul(
+                            score[:, tokens], shift_lo[:, b : b + 1].to_broadcast([P, P]), ident_b[:],
+                            start=False, stop=(s == BANK // P - 1),
+                        )
+                    if c == 0:
+                        nc.vector.tensor_scalar(
+                            neg_dist[kb][:, cols], score[:], 1.0 / 128.0, norm[:, kb : kb + 1], ALU.mult, ALU.subtract
+                        )
+                    else:
+                        nc.scalar.activation(
+                            neg_dist[kb][:, cols], score[:], ACT.Identity, scale=1.0 / 128.0, bias=neg_norm[:, kb : kb + 1]
+                        )
+
+        with (
+            tc.psum_pool(name="psum_last", bufs=2) as psum_last,
+            tc.psum_pool(name="psum_tiny", bufs=2) as psum_tiny,
+        ):
+            for c in range(PIECES):
+                cols = slice(c * PIECE, (c + 1) * PIECE)
+                piece_offsets = offsets[:, c * (PIECE // 16) : (c + 1) * (PIECE // 16)]
+                logits = work.tile([P, KB, PIECE], F32, name="logits")
+                for kb in range(KB):
+                    nc.vector.tensor_tensor(
+                        logits[:, kb, :], gate[kb][:].indirect(piece_offsets), neg_dist[kb][:, cols], ALU.add
+                    )
+                expo = work.tile([P, KB, PIECE], BF16, name="expo")
+                nc.scalar.activation(expo[:], logits[:], ACT.Exp)
+                denom = psum_tiny.tile([P, SUBS], F32, name="denom")
+                for s in range(SUBS):
+                    for kb in range(KB):
+                        nc.tensor.matmul(
+                            denom[:, s : s + 1], expo[:, kb, s * P : (s + 1) * P], ones_col[:], start=(kb == 0), stop=(kb == KB - 1)
+                        )
+                recip = small.tile([P, SUBS], F32, name="recip")
+                nc.vector.reciprocal(recip[:], denom[:])
+                last = psum_last.tile([P, 2, PIECE], F32, name="last")
+                for kb in range(KB):
+                    nc.tensor.matmul(last[:, 0, :], codes[:, kb, 0:D], expo[:, kb, :], start=(kb == 0), stop=(kb == KB - 1))
+                quant = work.tile([P, PIECE], F32, name="quant")
+                nc.scalar.copy(quant[:], last[:, 0, :])
+                for s in range(SUBS):
+                    nc.tensor.matmul(
+                        last[:, 1, s * P : (s + 1) * P], recip[:, s : s + 1].to_broadcast([P, P]), ident_f[:], start=True, stop=True
+                    )
+                result = work.tile([P, PIECE], F32, name="result")
+                nc.vector.tensor_tensor(result[:], quant[:], last[:, 1, :], ALU.mult)
+                nc.sync.dma_start(out[:, cols], result[:])

@@ -143,30 +143,30 @@ def tile_mirrorsystem_kernel(tc, z_real, z_imag, codebook, adj_t, offs, out):
                 nc.vector.tensor_scalar_mul(shift_hi[:, blocks], top[:], -1.0)
                 nc.vector.scalar_tensor_tensor(shift_lo[:, blocks], top[:], -1.0, shift_hi[:, blocks], ALU.mult, ALU.subtract)
 
-            for c in range(N // BANK):
-                cols = slice(c * BANK, (c + 1) * BANK)
+            for c in range(PIECES):
+                cols = slice(c * PIECE, (c + 1) * PIECE)
+                score = psum_score.tile([P, KB, PIECE], F32, name="score")
                 for kb in range(KB):
                     symbols = slice(kb * P, (kb + 1) * P)
-                    score = psum_score.tile([P, BANK], F32, name="score")
-                    nc.tensor.matmul(score[:], codes_t[:, 0, symbols], zr[:, cols], start=True, stop=False)
-                    nc.tensor.matmul(score[:], codes_t[:, 1, symbols], zi[:, cols], start=False, stop=False)
-                    for s in range(BANK // P):
-                        b = c * (BANK // P) + s
+                    nc.tensor.matmul(score[:, kb, :], codes_t[:, 0, symbols], zr[:, cols], start=True, stop=False)
+                    nc.tensor.matmul(score[:, kb, :], codes_t[:, 1, symbols], zi[:, cols], start=False, stop=False)
+                    for s in range(SUBS):
+                        b = c * SUBS + s
                         tokens = slice(s * P, (s + 1) * P)
                         nc.tensor.matmul(
-                            score[:, tokens], shift_hi[:, b : b + 1].to_broadcast([P, P]), ident_b[:], start=False, stop=False
+                            score[:, kb, tokens], shift_hi[:, b : b + 1].to_broadcast([P, P]), ident_b[:], start=False, stop=False
                         )
                         nc.tensor.matmul(
-                            score[:, tokens], shift_lo[:, b : b + 1].to_broadcast([P, P]), ident_b[:],
-                            start=False, stop=(s == BANK // P - 1),
+                            score[:, kb, tokens], shift_lo[:, b : b + 1].to_broadcast([P, P]), ident_b[:],
+                            start=False, stop=(s == SUBS - 1),
                         )
-                    if c == 0:
+                    if c < PIECES // 2:
                         nc.vector.tensor_scalar(
-                            neg_dist[kb][:, cols], score[:], 1.0 / 128.0, norm[:, kb : kb + 1], ALU.mult, ALU.subtract
+                            neg_dist[kb][:, cols], score[:, kb, :], 1.0 / 128.0, norm[:, kb : kb + 1], ALU.mult, ALU.subtract
                         )
                     else:
                         nc.scalar.activation(
-                            neg_dist[kb][:, cols], score[:], ACT.Identity, scale=1.0 / 128.0, bias=neg_norm[:, kb : kb + 1]
+                            neg_dist[kb][:, cols], score[:, kb, :], ACT.Identity, scale=1.0 / 128.0, bias=neg_norm[:, kb : kb + 1]
                         )
 
         with (

@@ -197,9 +197,7 @@ def tile_mirrorsystem_kernel(tc, z_real, z_imag, codebook, adj_t, offs, out):
                 quant = work.tile([P, PIECE], F32, name="quant")
                 nc.scalar.copy(quant[:], last[:, 0, :])
                 for s in range(SUBS):
-                    nc.tensor.matmul(
-                        last[:, 1, s * P : (s + 1) * P], recip[:, s : s + 1].to_broadcast([P, P]), ident_f[:], start=True, stop=True
-                    )
+                    nc.tensor.transpose(last[:, 1, s * P : (s + 1) * P], recip[:, s : s + 1].to_broadcast([P, P]), ident_f[:])
                 result = work.tile([P, PIECE], F32, name="result")
                 nc.vector.tensor_tensor(result[:], quant[:], last[:, 1, :], ALU.mult)
                 nc.sync.dma_start(out[:, cols], result[:])

@@ -14,7 +14,6 @@ KB = K // P
 PIECE = 256
 PIECES = N // PIECE
 SUBS = PIECE // P
-BANK = 512
 HALF = N // 2
 COUNT = D * N
 UNBIAS = COUNT / (COUNT - 1.0)
@@ -29,7 +28,7 @@ def tile_mirrorsystem_kernel(tc, z_real, z_imag, codebook, adj_t, offs, out):
         tc.tile_pool(name="held", bufs=1) as held,
         tc.tile_pool(name="work", bufs=2) as work,
         tc.tile_pool(name="small", bufs=2) as small,
-        tc.psum_pool(name="psum_score", bufs=4) as psum_score,
+        tc.psum_pool(name="psum_score", bufs=PIECES) as psum_score,
     ):
         adj = held.tile([P, KB, K], F32, name="adj")
         nc.scalar.dma_start(adj[:], adj_t.rearrange("(b p) n -> p b n", p=P))
@@ -60,8 +59,7 @@ def tile_mirrorsystem_kernel(tc, z_real, z_imag, codebook, adj_t, offs, out):
 
         neg_dist = [held.tile([P, N], F32, name=f"neg_dist{kb}") for kb in range(KB)]
         neg_var = held.tile([P, 1], F32, name="neg_var")
-        shift_hi = held.tile([P, N // P], BF16, name="shift_hi")
-        shift_lo = held.tile([P, N // P], BF16, name="shift_lo")
+        neg_top = held.tile([P, N // P], F32, name="neg_top")
         with tc.psum_pool(name="psum_pre", bufs=1) as psum_pre:
             code_sq = held.tile([P, KB, 2 * D], F32, name="code_sq")
             norm = held.tile([P, KB], F32, name="norm")
@@ -79,10 +77,8 @@ def tile_mirrorsystem_kernel(tc, z_real, z_imag, codebook, adj_t, offs, out):
             nc.vector.tensor_copy(codes_t[:], codes_t_ps[:])
             neg_norm = held.tile([P, KB], F32, name="neg_norm")
             nc.vector.tensor_scalar_mul(neg_norm[:], norm[:], -1.0)
-            norm_hi = held.tile([P, KB], BF16, name="norm_hi")
-            nc.vector.tensor_scalar_mul(norm_hi[:], norm[:], -128.0)
-            norm_lo = held.tile([P, KB], BF16, name="norm_lo")
-            nc.vector.scalar_tensor_tensor(norm_lo[:], norm[:], -128.0, norm_hi[:], ALU.mult, ALU.subtract)
+            norm_scaled = held.tile([P, KB], F32, name="norm_scaled")
+            nc.vector.tensor_scalar_mul(norm_scaled[:], norm[:], -128.0)
 
             sig = held.tile([P, KB, K], F32, name="sig")
             nc.scalar.activation(sig[:], adj[:], ACT.Sigmoid)
@@ -131,17 +127,10 @@ def tile_mirrorsystem_kernel(tc, z_real, z_imag, codebook, adj_t, offs, out):
                     for kb in range(KB):
                         symbols = slice(kb * P, (kb + 1) * P)
                         nc.tensor.matmul(
-                            score_t[:, s, symbols], norm_hi[:, kb : kb + 1].to_broadcast([P, P]), ident_b[:],
-                            start=False, stop=False,
+                            score_t[:, s, symbols], norm_scaled[:, kb : kb + 1].to_broadcast([P, P]), ident_f[:],
+                            is_transpose=True, start=False, stop=(kb == KB - 1),
                         )
-                        nc.tensor.matmul(
-                            score_t[:, s, symbols], norm_lo[:, kb : kb + 1].to_broadcast([P, P]), ident_b[:],
-                            start=False, stop=(kb == KB - 1),
-                        )
-                top = small.tile([P, SUBS], F32, name="top")
-                nc.vector.tensor_reduce(top[:], score_t[:], AX.X, ALU.max)
-                nc.vector.tensor_scalar_mul(shift_hi[:, blocks], top[:], -1.0)
-                nc.vector.scalar_tensor_tensor(shift_lo[:, blocks], top[:], -1.0, shift_hi[:, blocks], ALU.mult, ALU.subtract)
+                nc.vector.tensor_reduce(neg_top[:, blocks], score_t[:], AX.X, ALU.max, negate=True)
 
             for c in range(PIECES):
                 cols = slice(c * PIECE, (c + 1) * PIECE)
@@ -154,11 +143,8 @@ def tile_mirrorsystem_kernel(tc, z_real, z_imag, codebook, adj_t, offs, out):
                         b = c * SUBS + s
                         tokens = slice(s * P, (s + 1) * P)
                         nc.tensor.matmul(
-                            score[:, kb, tokens], shift_hi[:, b : b + 1].to_broadcast([P, P]), ident_b[:], start=False, stop=False
-                        )
-                        nc.tensor.matmul(
-                            score[:, kb, tokens], shift_lo[:, b : b + 1].to_broadcast([P, P]), ident_b[:],
-                            start=False, stop=(s == SUBS - 1),
+                            score[:, kb, tokens], neg_top[:, b : b + 1].to_broadcast([P, P]), ident_f[:],
+                            is_transpose=True, start=False, stop=(s == SUBS - 1),
                         )
                     if c < PIECES // 2:
                         nc.vector.tensor_scalar(

import concourse.mybir as mybir
from concourse.masks import make_identity

F32 = mybir.dt.float32
BF16 = mybir.dt.bfloat16
U16 = mybir.dt.uint16
ALU = mybir.AluOpType
ACT = mybir.ActivationFunctionType
AX = mybir.AxisListType

P = 128
D, K, N = 128, 256, 1024
KB = K // P
PIECE = 256
PIECES = N // PIECE
SUBS = PIECE // P
HALF = N // 2
COUNT = D * N
UNBIAS = COUNT / (COUNT - 1.0)
EULER = 2.718281828459045

FLOPS = 2 * K * 2 * D * N + 2 * K * D * N


def tile_mirrorsystem_kernel(tc, z_real, z_imag, codebook, adj_t, offs, out):
    nc = tc.nc
    with (
        tc.tile_pool(name="held", bufs=1) as held,
        tc.tile_pool(name="work", bufs=2) as work,
        tc.tile_pool(name="small", bufs=2) as small,
        tc.psum_pool(name="psum_score", bufs=PIECES) as psum_score,
    ):
        adj = held.tile([P, KB, K], F32, name="adj")
        nc.scalar.dma_start(adj[:], adj_t.rearrange("(b p) n -> p b n", p=P))
        codes = held.tile([P, KB, 2 * D], BF16, name="codes")
        nc.sync.dma_start(codes[:], codebook.rearrange("(b p) e -> p b e", p=P))
        zr = held.tile([P, N], BF16, name="zr")
        zi = held.tile([P, N], BF16, name="zi")
        for h in range(2):
            cols = slice(h * HALF, (h + 1) * HALF)
            nc.sync.dma_start(zr[:, cols], z_real[:, cols])
            nc.sync.dma_start(zi[:, cols], z_imag[:, cols])
        offsets = held.tile([P, N // 16], U16, name="offsets")
        nc.sync.dma_start(offsets[:], offs)

        euler = held.tile([P, 1], F32, name="euler")
        nc.vector.memset(euler[:], EULER**UNBIAS)
        averager = held.tile([P, P], F32, name="averager")
        nc.vector.memset(averager[:], 1.0 / COUNT)
        ones_col = held.tile([P, 1], BF16, name="ones_col")
        nc.vector.memset(ones_col[:], 1.0)
        ident_b = held.tile([P, P], BF16, name="ident_b")
        make_identity(nc, ident_b[:])
        ident_f = held.tile([P, P], F32, name="ident_f")
        make_identity(nc, ident_f[:])

        warm = held.tile([P, 4], F32, name="warm")
        nc.scalar.activation(warm[:, 0:1], euler[:], ACT.Sigmoid)

        neg_dist = [held.tile([P, N], F32, name=f"neg_dist{kb}") for kb in range(KB)]
        neg_var = held.tile([P, 1], F32, name="neg_var")
        neg_top = held.tile([P, N // P], F32, name="neg_top")
        with tc.psum_pool(name="psum_pre", bufs=1) as psum_pre:
            code_sq = held.tile([P, KB, 2 * D], F32, name="code_sq")
            norm = held.tile([P, KB], F32, name="norm")
            for kb in range(KB):
                nc.scalar.activation(
                    code_sq[:, kb, :], codes[:, kb, :], ACT.Square, scale=1.0 / 16.0, accum_out=norm[:, kb : kb + 1]
                )
            codes_t_ps = psum_pre.tile([P, 2, K], BF16, name="codes_t_ps", tag="wide", bufs=3)
            for kb in range(KB):
                for half in range(2):
                    nc.tensor.transpose(
                        codes_t_ps[:, half, kb * P : (kb + 1) * P], codes[:, kb, half * D : (half + 1) * D], ident_b[:]
                    )
            codes_t = held.tile([P, 2, K], BF16, name="codes_t")
            nc.vector.tensor_copy(codes_t[:], codes_t_ps[:])
            neg_norm = held.tile([P, KB], F32, name="neg_norm")
            nc.vector.tensor_scalar_mul(neg_norm[:], norm[:], -1.0)
            norm_scaled = held.tile([P, KB], F32, name="norm_scaled")
            nc.vector.tensor_scalar_mul(norm_scaled[:], norm[:], -128.0)

            sig = held.tile([P, KB, K], F32, name="sig")
            nc.scalar.activation(sig[:], adj[:], ACT.Sigmoid)
            nc.scalar.activation(warm[:, 1:2], sig[:, 0, 0:1], ACT.Sqrt)

            sq_r = held.tile([P, N], F32, name="sq_r")
            sq_i = held.tile([P, N], F32, name="sq_i")
            mag_sq = held.tile([P, N], F32, name="mag_sq")
            mag = held.tile([P, N], F32, name="mag")
            sums = [held.tile([P, 2], F32, name=f"sums{h}") for h in range(2)]
            means_ps = psum_pre.tile([P, 2], F32, name="means_ps")
            for h in range(2):
                cols = slice(h * HALF, (h + 1) * HALF)
                nc.gpsimd.tensor_tensor(sq_r[:, cols], zr[:, cols], zr[:, cols], ALU.mult)
                nc.vector.tensor_tensor(sq_i[:, cols], zi[:, cols], zi[:, cols], ALU.mult)
            for h in range(2):
                cols = slice(h * HALF, (h + 1) * HALF)
                nc.vector.scalar_tensor_tensor(
                    mag_sq[:, cols], sq_r[:, cols], 1.0, sq_i[:, cols], ALU.mult, ALU.add, accum_out=sums[h][:, 0:1]
                )
                nc.scalar.activation(mag[:, cols], mag_sq[:, cols], ACT.Sqrt, accum_out=sums[h][:, 1:2])
                nc.tensor.matmul(means_ps[:], averager[:], sums[h][:], start=(h == 0), stop=(h == 1))
            nc.scalar.activation(warm[:, 2:3], sums[1][:, 1:2], ACT.Ln, bias=sums[0][:, 1:2])
            nc.vector.tensor_scalar(neg_var[:], means_ps[:, 1:2], means_ps[:, 1:2], means_ps[:, 0:1], ALU.mult, ALU.subtract)

            exp_neg = held.tile([P, 1], F32, name="exp_neg")
            nc.gpsimd.tensor_tensor(exp_neg[:], euler[:], neg_var[:], ALU.pow)
            tenth_var = held.tile([P, 1], F32, name="tenth_var")
            nc.vector.tensor_scalar_mul(tenth_var[:], neg_var[:], -0.1 * UNBIAS)
            log_term = held.tile([P, 1], F32, name="log_term")
            nc.scalar.activation(log_term[:], exp_neg[:], ACT.Ln, bias=1.0)
            nc.scalar.activation(warm[:, 3:4], log_term[:], ACT.Exp)
            gam = held.tile([P, 1], F32, name="gam")
            nc.vector.tensor_scalar(gam[:], log_term[:], 0.1, tenth_var[:, 0:1], ALU.mult, ALU.add)
            gate = [held.tile([P, K], F32, name=f"gate{kb}") for kb in range(KB)]
            for kb in range(KB):
                nc.vector.tensor_scalar(gate[kb][:], sig[:, kb, :], 1.0, gam[:, 0:1], ALU.subtract, ALU.mult)

            for c in range(PIECES):
                blocks = slice(c * SUBS, (c + 1) * SUBS)
                score_t = psum_pre.tile([P, SUBS, K], F32, name="score_t", tag="wide", bufs=3)
                for s in range(SUBS):
                    tokens = slice((c * SUBS + s) * P, (c * SUBS + s + 1) * P)
                    nc.tensor.matmul(score_t[:, s, :], zr[:, tokens], codes_t[:, 0, :], start=True, stop=False)
                    nc.tensor.matmul(score_t[:, s, :], zi[:, tokens], codes_t[:, 1, :], start=False, stop=False)
                    for kb in range(KB):
                        symbols = slice(kb * P, (kb + 1) * P)
                        nc.tensor.matmul(
                            score_t[:, s, symbols], norm_scaled[:, kb : kb + 1].to_broadcast([P, P]), ident_f[:],
                            is_transpose=True, start=False, stop=(kb == KB - 1),
                        )
                nc.vector.tensor_reduce(neg_top[:, blocks], score_t[:], AX.X, ALU.max, negate=True)

            for c in range(PIECES):
                cols = slice(c * PIECE, (c + 1) * PIECE)
                score = psum_score.tile([P, KB, PIECE], F32, name="score")
                for kb in range(KB):
                    symbols = slice(kb * P, (kb + 1) * P)
                    nc.tensor.matmul(score[:, kb, :], codes_t[:, 0, symbols], zr[:, cols], start=True, stop=False)
                    nc.tensor.matmul(score[:, kb, :], codes_t[:, 1, symbols], zi[:, cols], start=False, stop=False)
                    for s in range(SUBS):
                        b = c * SUBS + s
                        tokens = slice(s * P, (s + 1) * P)
                        nc.tensor.matmul(
                            score[:, kb, tokens], neg_top[:, b : b + 1].to_broadcast([P, P]), ident_f[:],
                            is_transpose=True, start=False, stop=(s == SUBS - 1),
                        )
                    if c < PIECES // 2:
                        nc.vector.tensor_scalar(
                            neg_dist[kb][:, cols], score[:, kb, :], 1.0 / 128.0, norm[:, kb : kb + 1], ALU.mult, ALU.subtract
                        )
                    else:
                        nc.scalar.activation(
                            neg_dist[kb][:, cols], score[:, kb, :], ACT.Identity, scale=1.0 / 128.0, bias=neg_norm[:, kb : kb + 1]
                        )

        with (
            tc.psum_pool(name="psum_last", bufs=2) as psum_last,
            tc.psum_pool(name="psum_tiny", bufs=2) as psum_tiny,
        ):
            for c in range(PIECES):
                cols = slice(c * PIECE, (c + 1) * PIECE)
                piece_offsets = offsets[:, c * (PIECE // 16) : (c + 1) * (PIECE // 16)]
                logits = work.tile([P, KB, PIECE], F32, name="logits")
                for kb in range(KB):
                    nc.vector.tensor_tensor(
                        logits[:, kb, :], gate[kb][:].indirect(piece_offsets), neg_dist[kb][:, cols], ALU.add
                    )
                expo = work.tile([P, KB, PIECE], BF16, name="expo")
                nc.scalar.activation(expo[:], logits[:], ACT.Exp)
                denom = psum_tiny.tile([P, SUBS], F32, name="denom")
                for s in range(SUBS):
                    for kb in range(KB):
                        nc.tensor.matmul(
                            denom[:, s : s + 1], expo[:, kb, s * P : (s + 1) * P], ones_col[:], start=(kb == 0), stop=(kb == KB - 1)
                        )
                recip = small.tile([P, SUBS], F32, name="recip")
                nc.vector.reciprocal(recip[:], denom[:])
                last = psum_last.tile([P, 2, PIECE], F32, name="last")
                for kb in range(KB):
                    nc.tensor.matmul(last[:, 0, :], codes[:, kb, 0:D], expo[:, kb, :], start=(kb == 0), stop=(kb == KB - 1))
                quant = work.tile([P, PIECE], F32, name="quant")
                nc.scalar.copy(quant[:], last[:, 0, :])
                for s in range(SUBS):
                    nc.tensor.transpose(last[:, 1, s * P : (s + 1) * P], recip[:, s : s + 1].to_broadcast([P, P]), ident_f[:])
                result = work.tile([P, PIECE], F32, name="result")
                nc.vector.tensor_tensor(result[:], quant[:], last[:, 1, :], ALU.mult)
                nc.sync.dma_start(out[:, cols], result[:])
